import numpy as np
import ml_dtypes


def mxq(x, axis, fmt="e4m3"):
    dtype, down = {"e4m3": (ml_dtypes.float8_e4m3fn, 7), "e5m2": (ml_dtypes.float8_e5m2, 14)}[fmt]
    v = np.moveaxis(np.asarray(x, np.float32).astype(ml_dtypes.bfloat16).astype(np.float64), axis, -1)
    blocks = v.reshape(v.shape[:-1] + (-1, 32))
    amax = np.abs(blocks).max(-1, keepdims=True)
    byte = np.maximum(np.where(amax > 0, np.frexp(amax)[1] - 1 + 127, 0) - down, 1)
    scale = np.exp2(byte - 127.0)
    codes = (blocks / scale).astype(np.float32).astype(dtype).astype(np.float64)
    return np.moveaxis((codes * scale).reshape(v.shape), -1, axis)


WIDE = False


def mx_kscale(k):
    if not WIDE:
        return np.ones(k)
    levels = np.array([10, -10, 5, -5, 0])
    a = np.random.permutation(np.resize(levels, k // 512 * 4)).reshape(k // 512, 4)
    idx = np.arange(k)
    return np.exp2(a[idx // 512, idx % 128 // 32])


BF16 = ml_dtypes.bfloat16


def bf(x):
    return np.asarray(x, np.float32).astype(BF16)


def f64(x):
    return np.asarray(x).astype(np.float64)


B, H, S, D = 8, 2, 512, 256


def setup_inputs():
    s = mx_kscale(S)
    return {"mat1": bf(np.random.standard_normal((B, H, S, D))),
            "mat2": bf(np.random.standard_normal((B, H, S, D))),
            "mat3": bf(np.random.standard_normal((B, H, S, D)) * 3.0 * s.max() / s[:, None]),
            "bias": bf((np.random.standard_normal((S, S)) + np.log(s))[None, None])}


def reference(mat1, mat2, mat3, bias):
    s = (f64(mat1) @ f64(mat2).transpose(0, 1, 3, 2)) / np.sqrt(D) + f64(bias)
    e = np.exp(s - s.max(-1, keepdims=True))
    p = e / e.sum(-1, keepdims=True)
    return mxq(p, 3, "e4m3") @ mxq(f64(mat3), 2, "e4m3")

@@ -1,0 +1,232 @@
+from contextlib import ExitStack
+
+import concourse.mybir as mybir
+from concourse.masks import make_identity
+
+F32 = mybir.dt.float32
+BF16 = mybir.dt.bfloat16
+U32 = mybir.dt.uint32
+U8 = mybir.dt.uint8
+FP8X4 = mybir.dt.float8_e4m3fn_x4
+ALU = mybir.AluOpType
+ACT = mybir.ActivationFunctionType
+AX = mybir.AxisListType
+
+P = 128
+NB, NHB, S, D = 8, 2, 512, 256
+NH = NB * NHB
+NT = S // P
+FLOPS = 2 * 2 * NH * S * S * D
+
+PE_BIAS = ()
+NORM_ENGINE = "g"
+VREG_ENGINE = "v"
+QK_COPY = ("s", "s")
+P_COPY = ("s", "s")
+O_COPY = ("s", "s")
+PINNED = False
+
+
+def tile_fake_sd_mha_model_pa_t_kernel(tc, mat1, mat2, mat3, bias, out):
+    nc = tc.nc
+
+    def copy_on(engine, dst, src):
+        if engine == "s":
+            nc.scalar.copy(out=dst, in_=src)
+        else:
+            nc.vector.tensor_copy(out=dst, in_=src)
+
+    with ExitStack() as ctx:
+        if PINNED:
+            ctx.enter_context(tc.manual_schedule())
+        const = ctx.enter_context(tc.tile_pool(name="const", bufs=1))
+        raw = ctx.enter_context(tc.tile_pool(name="raw", bufs=NH))
+        work = ctx.enter_context(tc.tile_pool(name="work", bufs=3))
+        small = ctx.enter_context(tc.tile_pool(name="small", bufs=8))
+        psum = ctx.enter_context(tc.psum_pool(name="psum", bufs=2))
+
+        q_raw, k_raw, v_raw = [], [], []
+        bias_raw = const.tile([P, NT, S], BF16, name="bias_raw")
+        for h in range(NH):
+            b, hh = divmod(h, NHB)
+            qr = raw.tile([P, NT * D], BF16, name="qr", tag="qr")
+            nc.sync.dma_start(out=qr[:], in_=mat1[b, hh].rearrange("(p j) d -> p (j d)", j=NT))
+            kr = raw.tile([P, NT * D], BF16, name="kr", tag="kr")
+            nc.sync.dma_start(out=kr[:], in_=mat2[b, hh].rearrange("(p j) d -> p (j d)", j=NT))
+            if h == 0:
+                nc.sync.dma_start(
+                    out=bias_raw[:].rearrange("p j k -> p (j k)"),
+                    in_=bias[0, 0].rearrange("(p j) k -> p (j k)", j=NT),
+                )
+            vr = raw.tile([P, NT, D], BF16, name="vr", tag="vr")
+            nc.sync.dma_start(
+                out=vr[:].rearrange("p t d -> p (t d)"),
+                in_=mat3[b, hh].rearrange("(p t) d -> p (t d)", t=NT),
+            )
+            q_raw.append(qr)
+            k_raw.append(kr)
+            v_raw.append(vr)
+
+        ident_f = const.tile([P, P], F32, name="ident_f")
+        make_identity(nc, ident_f[:])
+        ident_b = const.tile([P, P], BF16, name="ident_b")
+        make_identity(nc, ident_b[:])
+        warm = const.tile([P, 1], F32, name="warm")
+        nc.vector.memset(warm[:], 0.0)
+        nc.scalar.activation(out=warm[:], in_=warm[:], func=ACT.Exp)
+
+        bias_perm = const.tile([P, NT, NT, P], BF16, name="bias_perm")
+        for j in range(NT):
+            nc.vector.tensor_copy(
+                out=bias_perm[:, j], in_=bias_raw[:, j, :].rearrange("p (c t) -> p t c", t=NT)
+            )
+        bias_t = None
+        if PE_BIAS:
+            bias_t = const.tile([P, NT, NT, P], F32, name="bias_t")
+            for j in PE_BIAS:
+                bt_ps = psum.tile([P, 2, NT, P], BF16, name="bt_ps", tag="pt")
+                for t in range(NT):
+                    nc.tensor.transpose(bt_ps[:, 0, t, :], bias_perm[:, j, t, :], ident_b[:])
+                nc.vector.tensor_scalar_mul(out=bias_t[:, j], in0=bt_ps[:, 0], scalar1=16.0)
+
+        qT, kT, v_q, p_tiles, g_tiles = {}, {}, {}, {}, {}
+
+        def prep_qk(h):
+            for which, (src, store) in enumerate(((q_raw[h], qT), (k_raw[h], kT))):
+                words = src[:].bitcast(F32)
+                tp = psum.tile([P, S], F32, name="tp", tag="tp")
+                for j in range(NT):
+                    nc.tensor.transpose(tp[:, j * P : (j + 1) * P], words[:, j * P : (j + 1) * P], ident_f[:])
+                xt = work.tile([P, S], F32, name="xt", tag="xt%d" % which)
+                copy_on(QK_COPY[which], xt[:], tp[:])
+                store[h] = xt[:].bitcast(BF16).rearrange("w (c e) -> w c e", e=2)
+
+        def prep_v(h):
+            vg = work.tile([P, D, NT], BF16, name="vg", tag="vg", align_bytes=64)
+            dst = vg[:].rearrange("p (c i) t -> p c t i", i=4)
+            src = v_raw[h][:].rearrange("p t (c i) -> p c t i", i=4)
+            if VREG_ENGINE == "g":
+                nc.gpsimd.tensor_scalar(out=dst, in0=src, scalar1=1.0, scalar2=0.0, op0=ALU.mult, op1=ALU.add)
+            else:
+                nc.vector.tensor_copy(out=dst, in_=src)
+            vc = work.tile([P, D], U32, name="vc", tag="vc", align_bytes=64)
+            vs = work.tile([P, D], U8, name="vs", tag="vs", align_bytes=64)
+            nc.vector.quantize_mx(
+                out=vc[:].bitcast(FP8X4), scales=vs[:], in_=vg[:].rearrange("p d t -> p (d t)")
+            )
+            v_q[h] = (vc, vs)
+
+        def scores(h, j):
+            s_ps = psum.tile([P, S], F32, name="s_ps", tag="s", bufs=3)
+            on_pe = j in PE_BIAS
+            for e in range(2):
+                nc.tensor.matmul(
+                    s_ps[:],
+                    lhsT=qT[h][:, j * P : (j + 1) * P, e],
+                    rhs=kT[h][:, :, e],
+                    start=(e == 0),
+                    stop=(e == 1 and not on_pe),
+                )
+            nm = small.tile([P, 1], F32, name="nm", tag="nm")
+            ssum = small.tile([P, 1], F32, name="ssum", tag="ssum")
+            e_sb = work.tile([P, S], F32, name="e_sb", tag="e", bufs=4)
+            if on_pe:
+                for t in range(NT):
+                    nc.tensor.matmul(
+                        s_ps[:, t * P : (t + 1) * P],
+                        lhsT=bias_t[:, j, t, :],
+                        rhs=ident_f[:],
+                        is_transpose=True,
+                        start=False,
+                        stop=(t == NT - 1),
+                    )
+                nm16 = small.tile([P, 1], F32, name="nm16", tag="nm16")
+                nc.vector.tensor_reduce(out=nm16[:], in_=s_ps[:], axis=AX.X, op=ALU.max, negate=True)
+                nc.vector.tensor_scalar_mul(out=nm[:], in0=nm16[:], scalar1=1.0 / 16.0)
+                nc.scalar.activation(
+                    out=e_sb[:], in_=s_ps[:], func=ACT.Exp, bias=nm[:], scale=1.0 / 16.0, accum_out=ssum[:]
+                )
+            else:
+                z = work.tile([P, S], F32, name="z", tag="z", bufs=3)
+                nc.vector.scalar_tensor_tensor(
+                    out=z[:],
+                    in0=s_ps[:],
+                    scalar=1.0 / 16.0,
+                    in1=bias_perm[:, j].rearrange("p t c -> p (t c)"),
+                    op0=ALU.mult,
+                    op1=ALU.add,
+                )
+                nc.vector.tensor_reduce(out=nm[:], in_=z[:], axis=AX.X, op=ALU.max, negate=True)
+                nc.scalar.activation(
+                    out=e_sb[:], in_=z[:], func=ACT.Exp, bias=nm[:], scale=1.0, accum_out=ssum[:]
+                )
+            r = small.tile([P, 1], F32, name="r", tag="r")
+            nc.vector.reciprocal(r[:], ssum[:])
+            p_sb = work.tile([P, S], BF16, name="p_sb", tag="p", bufs=8)
+            if NORM_ENGINE == "g":
+                nc.gpsimd.tensor_scalar(
+                    out=p_sb[:], in0=e_sb[:], scalar1=r[:], scalar2=0.0, op0=ALU.mult, op1=ALU.add
+                )
+            else:
+                nc.vector.tensor_scalar_mul(out=p_sb[:], in0=e_sb[:], scalar1=r[:])
+            p_tiles[(h, j)] = p_sb
+
+        pt_now = {}
+
+        def transpose_p(h, j):
+            a = j % 2
+            if a == 0:
+                pt_now[h] = psum.tile([P, 2, NT, P], BF16, name="pt_ps", tag="pt")
+            if j == 0:
+                g_tiles[h] = work.tile([P, NT, P, NT], BF16, name="g", tag="g", align_bytes=64)
+            pt_ps = pt_now[h]
+            for t in range(NT):
+                nc.tensor.transpose(pt_ps[:, a, t, :], p_tiles[(h, j)][:, t * P : (t + 1) * P], ident_b[:])
+            if a == 1:
+                copy_on(
+                    P_COPY[j // 2],
+                    g_tiles[h][:, j - 1 : j + 1],
+                    pt_ps[:].rearrange("p a t q -> p a q t"),
+                )
+
+        def finish(h):
+            b, hh = divmod(h, NHB)
+            pc = work.tile([P, S], U32, name="pc", tag="pc", align_bytes=64)
+            ps = work.tile([P, S], U8, name="ps", tag="ps", align_bytes=64)
+            nc.vector.quantize_mx(
+                out=pc[:].bitcast(FP8X4), scales=ps[:], in_=g_tiles[h][:].rearrange("p j q t -> p (j q t)")
+            )
+            vc, vs = v_q[h]
+            o_sb = work.tile([P, NT, D], F32, name="o_sb", tag="o", bufs=6)
+            for pair in range(2):
+                o_ps = psum.tile([P, 2, D], F32, name="o_ps", tag="o", bufs=1)
+                for a in range(2):
+                    j = 2 * pair + a
+                    nc.tensor.matmul_mx(
+                        out=o_ps[:, a, :],
+                        lhsT=pc[:, j * P : (j + 1) * P].bitcast(FP8X4),
+                        lhsT_scale=ps[:, j * P : (j + 1) * P],
+                        rhs=vc[:].bitcast(FP8X4),
+                        rhs_scale=vs[:],
+                        start=True,
+                        stop=True,
+                    )
+                copy_on(O_COPY[pair], o_sb[:, 2 * pair : 2 * pair + 2, :], o_ps[:])
+            nc.sync.dma_start(
+                out=out[b, hh].rearrange("(p j) d -> p (j d)", j=NT),
+                in_=o_sb[:].rearrange("p j d -> p (j d)"),
+            )
+
+        prep_qk(0)
+        for h in range(NH + 1):
+            if h + 1 < NH:
+                prep_qk(h + 1)
+            if h < NH:
+                prep_v(h)
+            for j in range(NT):
+                if h < NH:
+                    scores(h, j)
+                if h >= 1:
+                    transpose_p(h - 1, j)
+            if h >= 1:
+                finish(h - 1)

@@ -16,15 +16,18 @@ P = 128
 NB, NHB, S, D = 8, 2, 512, 256
 NH = NB * NHB
 NT = S // P
+NSTEP = NH * NT
 FLOPS = 2 * 2 * NH * S * S * D
 
-PE_BIAS = ()
+PE_BIAS = (0, 1, 2, 3)
 NORM_ENGINE = "g"
 VREG_ENGINE = "v"
-QK_COPY = ("s", "s")
+QK_COPY = ("s", "v")
 P_COPY = ("s", "s")
-O_COPY = ("s", "s")
-PINNED = False
+O_COPY = ("v", "v")
+PINNED = True
+PREFETCH = 3
+L_MAX, L_EXP, L_NORM, L_PT, L_PCOPY, L_QUANT, L_MX, L_OCOPY, L_STORE = 1, 2, 3, 5, 6, 7, 8, 9, 10
 
 
 def tile_fake_sd_mha_model_pa_t_kernel(tc, mat1, mat2, mat3, bias, out):
@@ -40,32 +43,194 @@ def tile_fake_sd_mha_model_pa_t_kernel(tc, mat1, mat2, mat3, bias, out):
         if PINNED:
             ctx.enter_context(tc.manual_schedule())
         const = ctx.enter_context(tc.tile_pool(name="const", bufs=1))
-        raw = ctx.enter_context(tc.tile_pool(name="raw", bufs=NH))
+        raw = ctx.enter_context(tc.tile_pool(name="raw", bufs=PREFETCH + 2))
         work = ctx.enter_context(tc.tile_pool(name="work", bufs=3))
         small = ctx.enter_context(tc.tile_pool(name="small", bufs=8))
         psum = ctx.enter_context(tc.psum_pool(name="psum", bufs=2))
 
-        q_raw, k_raw, v_raw = [], [], []
-        bias_raw = const.tile([P, NT, S], BF16, name="bias_raw")
-        for h in range(NH):
+        q_raw, k_raw, v_raw = {}, {}, {}
+        tp_now, qT, kT, vg_now, v_q = {}, {}, {}, {}, {}
+        s_now, z_now, nm_now, e_now, sum_now, p_now = {}, {}, {}, {}, {}, {}
+        pt_now, g_now, pq_now, ops_now, osb_now = {}, {}, {}, {}, {}
+
+        def load(h):
             b, hh = divmod(h, NHB)
-            qr = raw.tile([P, NT * D], BF16, name="qr", tag="qr")
-            nc.sync.dma_start(out=qr[:], in_=mat1[b, hh].rearrange("(p j) d -> p (j d)", j=NT))
-            kr = raw.tile([P, NT * D], BF16, name="kr", tag="kr")
-            nc.sync.dma_start(out=kr[:], in_=mat2[b, hh].rearrange("(p j) d -> p (j d)", j=NT))
-            if h == 0:
-                nc.sync.dma_start(
-                    out=bias_raw[:].rearrange("p j k -> p (j k)"),
-                    in_=bias[0, 0].rearrange("(p j) k -> p (j k)", j=NT),
-                )
-            vr = raw.tile([P, NT, D], BF16, name="vr", tag="vr")
+            q_raw[h] = raw.tile([P, NT * D], BF16, name="qr", tag="qr")
+            nc.sync.dma_start(out=q_raw[h][:], in_=mat1[b, hh].rearrange("(p j) d -> p (j d)", j=NT))
+            k_raw[h] = raw.tile([P, NT * D], BF16, name="kr", tag="kr")
+            nc.sync.dma_start(out=k_raw[h][:], in_=mat2[b, hh].rearrange("(p j) d -> p (j d)", j=NT))
+
+        def load_v(h):
+            b, hh = divmod(h, NHB)
+            v_raw[h] = raw.tile([P, NT, D], BF16, name="vr", tag="vr")
             nc.sync.dma_start(
-                out=vr[:].rearrange("p t d -> p (t d)"),
+                out=v_raw[h][:].rearrange("p t d -> p (t d)"),
                 in_=mat3[b, hh].rearrange("(p t) d -> p (t d)", t=NT),
             )
-            q_raw.append(qr)
-            k_raw.append(kr)
-            v_raw.append(vr)
+
+        def qk_transpose(h, which):
+            src = (q_raw, k_raw)[which][h]
+            words = src[:].bitcast(F32)
+            tp = psum.tile([P, S], F32, name="tp", tag="tp")
+            for j in range(NT):
+                nc.tensor.transpose(tp[:, j * P : (j + 1) * P], words[:, j * P : (j + 1) * P], ident_f[:])
+            tp_now[(h, which)] = tp
+
+        def qk_copy(h, which):
+            xt = work.tile([P, S], F32, name="xt", tag="xt%d" % which)
+            copy_on(QK_COPY[which], xt[:], tp_now[(h, which)][:])
+            (qT, kT)[which][h] = xt[:].bitcast(BF16).rearrange("w (c e) -> w c e", e=2)
+
+        def v_regroup(h):
+            vg = work.tile([P, D, NT], BF16, name="vg", tag="vg", align_bytes=64)
+            dst = vg[:].rearrange("p (c i) t -> p c t i", i=4)
+            src = v_raw[h][:].rearrange("p t (c i) -> p c t i", i=4)
+            if VREG_ENGINE == "g":
+                nc.gpsimd.tensor_scalar(out=dst, in0=src, scalar1=1.0, scalar2=0.0, op0=ALU.mult, op1=ALU.add)
+            else:
+                nc.vector.tensor_copy(out=dst, in_=src)
+            vg_now[h] = vg
+
+        def v_quant(h):
+            vc = work.tile([P, D], U32, name="vc", tag="vc", align_bytes=64)
+            vs = work.tile([P, D], U8, name="vs", tag="vs", align_bytes=64)
+            nc.vector.quantize_mx(
+                out=vc[:].bitcast(FP8X4), scales=vs[:], in_=vg_now[h][:].rearrange("p d t -> p (d t)")
+            )
+            v_q[h] = (vc, vs)
+
+        def mm(s, e):
+            h, j = divmod(s, NT)
+            if e == 0:
+                s_now[s] = psum.tile([P, S], F32, name="s_ps", tag="s", bufs=3)
+            nc.tensor.matmul(
+                s_now[s][:],
+                lhsT=qT[h][:, j * P : (j + 1) * P, e],
+                rhs=kT[h][:, :, e],
+                start=(e == 0),
+                stop=(e == 1 and j not in PE_BIAS),
+            )
+
+        def bias_add(s):
+            j = s % NT
+            if j in PE_BIAS:
+                for t in range(NT):
+                    nc.tensor.matmul(
+                        s_now[s][:, t * P : (t + 1) * P],
+                        lhsT=bias_t[:, j, t, :],
+                        rhs=ident_f[:],
+                        is_transpose=True,
+                        start=False,
+                        stop=(t == NT - 1),
+                    )
+
+        def row_max(s):
+            j = s % NT
+            z = work.tile([P, S], F32, name="z", tag="z")
+            nm = small.tile([P, 1], F32, name="nm", tag="nm")
+            if j in PE_BIAS:
+                nc.vector.tensor_scalar(
+                    out=z[:], in0=s_now[s][:], scalar1=-1.0 / 16.0, scalar2=None, op0=ALU.mult, op1=ALU.min,
+                    accum_out=nm[:],
+                )
+            else:
+                nc.vector.scalar_tensor_tensor(
+                    out=z[:],
+                    in0=s_now[s][:],
+                    scalar=1.0 / 16.0,
+                    in1=bias_perm[:, j].rearrange("p t c -> p (t c)"),
+                    op0=ALU.mult,
+                    op1=ALU.add,
+                )
+                nc.vector.tensor_reduce(out=nm[:], in_=z[:], axis=AX.X, op=ALU.max, negate=True)
+            z_now[s] = z
+            nm_now[s] = nm
+
+        def exp(s):
+            j = s % NT
+            e_sb = work.tile([P, S], F32, name="e_sb", tag="e")
+            ssum = small.tile([P, 1], F32, name="ssum", tag="ssum")
+            nc.scalar.activation(
+                out=e_sb[:],
+                in_=z_now[s][:],
+                func=ACT.Exp,
+                bias=nm_now[s][:],
+                scale=(-1.0 if j in PE_BIAS else 1.0),
+                accum_out=ssum[:],
+            )
+            e_now[s] = e_sb
+            sum_now[s] = ssum
+
+        def norm(s):
+            r = small.tile([P, 1], F32, name="r", tag="r")
+            nc.vector.reciprocal(r[:], sum_now[s][:])
+            p_sb = work.tile([P, S], BF16, name="p_sb", tag="p", bufs=5)
+            if NORM_ENGINE == "g":
+                nc.gpsimd.tensor_scalar(
+                    out=p_sb[:], in0=e_now[s][:], scalar1=r[:], scalar2=0.0, op0=ALU.mult, op1=ALU.add
+                )
+            else:
+                nc.vector.tensor_scalar_mul(out=p_sb[:], in0=e_now[s][:], scalar1=r[:])
+            p_now[s] = p_sb
+
+        def p_transpose(s):
+            u, a = divmod(s, 2)
+            if a == 0:
+                pt_now[u] = psum.tile([P, 2, NT, P], BF16, name="pt_ps", tag="pt")
+            for t in range(NT):
+                nc.tensor.transpose(pt_now[u][:, a, t, :], p_now[s][:, t * P : (t + 1) * P], ident_b[:])
+
+        def p_copy(u):
+            g = work.tile([P, 2, P, NT], BF16, name="g", tag="g", align_bytes=64)
+            copy_on(P_COPY[u % 2], g[:], pt_now[u][:].rearrange("p a t q -> p a q t"))
+            g_now[u] = g
+
+        def p_quant(u):
+            pc = work.tile([P, 2 * P], U32, name="pc", tag="pc", align_bytes=64)
+            ps = work.tile([P, 2 * P], U8, name="ps", tag="ps", align_bytes=64)
+            nc.vector.quantize_mx(
+                out=pc[:].bitcast(FP8X4), scales=ps[:], in_=g_now[u][:].rearrange("p a q t -> p (a q t)")
+            )
+            pq_now[u] = (pc, ps)
+
+        def mx(u):
+            pc, ps = pq_now[u]
+            vc, vs = v_q[u // 2]
+            o_ps = psum.tile([P, 2, D], F32, name="o_ps", tag="o", bufs=1)
+            for a in range(2):
+                nc.tensor.matmul_mx(
+                    out=o_ps[:, a, :],
+                    lhsT=pc[:, a * P : (a + 1) * P].bitcast(FP8X4),
+                    lhsT_scale=ps[:, a * P : (a + 1) * P],
+                    rhs=vc[:].bitcast(FP8X4),
+                    rhs_scale=vs[:],
+                    start=True,
+                    stop=True,
+                )
+            ops_now[u] = o_ps
+
+        def o_copy(u):
+            h, pair = divmod(u, 2)
+            if pair == 0:
+                osb_now[h] = work.tile([P, NT, D], F32, name="o_sb", tag="o")
+            copy_on(O_COPY[pair], osb_now[h][:, 2 * pair : 2 * pair + 2, :], ops_now[u][:])
+
+        def store(h):
+            b, hh = divmod(h, NHB)
+            nc.sync.dma_start(
+                out=out[b, hh].rearrange("(p j) d -> p (j d)", j=NT),
+                in_=osb_now[h][:].rearrange("p j d -> p (j d)"),
+            )
+
+        load(0)
+        bias_raw = const.tile([P, NT, S], BF16, name="bias_raw")
+        nc.sync.dma_start(
+            out=bias_raw[:].rearrange("p j k -> p (j k)"), in_=bias[0, 0].rearrange("(p j) k -> p (j k)", j=NT)
+        )
+        load_v(0)
+        for h in range(1, PREFETCH):
+            load(h)
+            load_v(h)
 
         ident_f = const.tile([P, P], F32, name="ident_f")
         make_identity(nc, ident_f[:])
@@ -75,158 +240,74 @@ def tile_fake_sd_mha_model_pa_t_kernel(tc, mat1, mat2, mat3, bias, out):
         nc.vector.memset(warm[:], 0.0)
         nc.scalar.activation(out=warm[:], in_=warm[:], func=ACT.Exp)
 
+        qk_transpose(0, 0)
+        qk_transpose(0, 1)
+        qk_copy(0, 0)
+        qk_copy(0, 1)
+
         bias_perm = const.tile([P, NT, NT, P], BF16, name="bias_perm")
+        bias_t = const.tile([P, NT, NT, P], F32, name="bias_t")
         for j in range(NT):
             nc.vector.tensor_copy(
                 out=bias_perm[:, j], in_=bias_raw[:, j, :].rearrange("p (c t) -> p t c", t=NT)
             )
-        bias_t = None
-        if PE_BIAS:
-            bias_t = const.tile([P, NT, NT, P], F32, name="bias_t")
-            for j in PE_BIAS:
+            if j in PE_BIAS:
                 bt_ps = psum.tile([P, 2, NT, P], BF16, name="bt_ps", tag="pt")
                 for t in range(NT):
                     nc.tensor.transpose(bt_ps[:, 0, t, :], bias_perm[:, j, t, :], ident_b[:])
                 nc.vector.tensor_scalar_mul(out=bias_t[:, j], in0=bt_ps[:, 0], scalar1=16.0)
 
-        qT, kT, v_q, p_tiles, g_tiles = {}, {}, {}, {}, {}
+        def tile_at(s, lag):
+            return s - lag if 0 <= s - lag < NSTEP else None
 
-        def prep_qk(h):
-            for which, (src, store) in enumerate(((q_raw[h], qT), (k_raw[h], kT))):
-                words = src[:].bitcast(F32)
-                tp = psum.tile([P, S], F32, name="tp", tag="tp")
-                for j in range(NT):
-                    nc.tensor.transpose(tp[:, j * P : (j + 1) * P], words[:, j * P : (j + 1) * P], ident_f[:])
-                xt = work.tile([P, S], F32, name="xt", tag="xt%d" % which)
-                copy_on(QK_COPY[which], xt[:], tp[:])
-                store[h] = xt[:].bitcast(BF16).rearrange("w (c e) -> w c e", e=2)
+        def pair_at(s, lag):
+            t = tile_at(s, lag)
+            return t // 2 if t is not None and t % 2 == 1 else None
 
-        def prep_v(h):
-            vg = work.tile([P, D, NT], BF16, name="vg", tag="vg", align_bytes=64)
-            dst = vg[:].rearrange("p (c i) t -> p c t i", i=4)
-            src = v_raw[h][:].rearrange("p t (c i) -> p c t i", i=4)
-            if VREG_ENGINE == "g":
-                nc.gpsimd.tensor_scalar(out=dst, in0=src, scalar1=1.0, scalar2=0.0, op0=ALU.mult, op1=ALU.add)
-            else:
-                nc.vector.tensor_copy(out=dst, in_=src)
-            vc = work.tile([P, D], U32, name="vc", tag="vc", align_bytes=64)
-            vs = work.tile([P, D], U8, name="vs", tag="vs", align_bytes=64)
-            nc.vector.quantize_mx(
-                out=vc[:].bitcast(FP8X4), scales=vs[:], in_=vg[:].rearrange("p d t -> p (d t)")
-            )
-            v_q[h] = (vc, vs)
+        for s in range(NSTEP + L_STORE + 1):
+            h, j = divmod(s, NT)
+            if j == 0 and h + PREFETCH < NH:
+                load(h + PREFETCH)
+                load_v(h + PREFETCH)
+            u_mx = pair_at(s, L_MX)
+            if s < NSTEP:
+                mm(s, 0)
+            if u_mx is not None:
+                mx(u_mx)
+            if s < NSTEP:
+                mm(s, 1)
+            t = tile_at(s, L_PT)
+            if t is not None:
+                p_transpose(t)
+            if s < NSTEP:
+                bias_add(s)
+            if h + 1 < NH and j < 2:
+                qk_transpose(h + 1, j)
 
-        def scores(h, j):
-            s_ps = psum.tile([P, S], F32, name="s_ps", tag="s", bufs=3)
-            on_pe = j in PE_BIAS
-            for e in range(2):
-                nc.tensor.matmul(
-                    s_ps[:],
-                    lhsT=qT[h][:, j * P : (j + 1) * P, e],
-                    rhs=kT[h][:, :, e],
-                    start=(e == 0),
-                    stop=(e == 1 and not on_pe),
-                )
-            nm = small.tile([P, 1], F32, name="nm", tag="nm")
-            ssum = small.tile([P, 1], F32, name="ssum", tag="ssum")
-            e_sb = work.tile([P, S], F32, name="e_sb", tag="e", bufs=4)
-            if on_pe:
-                for t in range(NT):
-                    nc.tensor.matmul(
-                        s_ps[:, t * P : (t + 1) * P],
-                        lhsT=bias_t[:, j, t, :],
-                        rhs=ident_f[:],
-                        is_transpose=True,
-                        start=False,
-                        stop=(t == NT - 1),
-                    )
-                nm16 = small.tile([P, 1], F32, name="nm16", tag="nm16")
-                nc.vector.tensor_reduce(out=nm16[:], in_=s_ps[:], axis=AX.X, op=ALU.max, negate=True)
-                nc.vector.tensor_scalar_mul(out=nm[:], in0=nm16[:], scalar1=1.0 / 16.0)
-                nc.scalar.activation(
-                    out=e_sb[:], in_=s_ps[:], func=ACT.Exp, bias=nm[:], scale=1.0 / 16.0, accum_out=ssum[:]
-                )
-            else:
-                z = work.tile([P, S], F32, name="z", tag="z", bufs=3)
-                nc.vector.scalar_tensor_tensor(
-                    out=z[:],
-                    in0=s_ps[:],
-                    scalar=1.0 / 16.0,
-                    in1=bias_perm[:, j].rearrange("p t c -> p (t c)"),
-                    op0=ALU.mult,
-                    op1=ALU.add,
-                )
-                nc.vector.tensor_reduce(out=nm[:], in_=z[:], axis=AX.X, op=ALU.max, negate=True)
-                nc.scalar.activation(
-                    out=e_sb[:], in_=z[:], func=ACT.Exp, bias=nm[:], scale=1.0, accum_out=ssum[:]
-                )
-            r = small.tile([P, 1], F32, name="r", tag="r")
-            nc.vector.reciprocal(r[:], ssum[:])
-            p_sb = work.tile([P, S], BF16, name="p_sb", tag="p", bufs=8)
-            if NORM_ENGINE == "g":
-                nc.gpsimd.tensor_scalar(
-                    out=p_sb[:], in0=e_sb[:], scalar1=r[:], scalar2=0.0, op0=ALU.mult, op1=ALU.add
-                )
-            else:
-                nc.vector.tensor_scalar_mul(out=p_sb[:], in0=e_sb[:], scalar1=r[:])
-            p_tiles[(h, j)] = p_sb
-
-        pt_now = {}
-
-        def transpose_p(h, j):
-            a = j % 2
-            if a == 0:
-                pt_now[h] = psum.tile([P, 2, NT, P], BF16, name="pt_ps", tag="pt")
-            if j == 0:
-                g_tiles[h] = work.tile([P, NT, P, NT], BF16, name="g", tag="g", align_bytes=64)
-            pt_ps = pt_now[h]
-            for t in range(NT):
-                nc.tensor.transpose(pt_ps[:, a, t, :], p_tiles[(h, j)][:, t * P : (t + 1) * P], ident_b[:])
-            if a == 1:
-                copy_on(
-                    P_COPY[j // 2],
-                    g_tiles[h][:, j - 1 : j + 1],
-                    pt_ps[:].rearrange("p a t q -> p a q t"),
-                )
-
-        def finish(h):
-            b, hh = divmod(h, NHB)
-            pc = work.tile([P, S], U32, name="pc", tag="pc", align_bytes=64)
-            ps = work.tile([P, S], U8, name="ps", tag="ps", align_bytes=64)
-            nc.vector.quantize_mx(
-                out=pc[:].bitcast(FP8X4), scales=ps[:], in_=g_tiles[h][:].rearrange("p j q t -> p (j q t)")
-            )
-            vc, vs = v_q[h]
-            o_sb = work.tile([P, NT, D], F32, name="o_sb", tag="o", bufs=6)
-            for pair in range(2):
-                o_ps = psum.tile([P, 2, D], F32, name="o_ps", tag="o", bufs=1)
-                for a in range(2):
-                    j = 2 * pair + a
-                    nc.tensor.matmul_mx(
-                        out=o_ps[:, a, :],
-                        lhsT=pc[:, j * P : (j + 1) * P].bitcast(FP8X4),
-                        lhsT_scale=ps[:, j * P : (j + 1) * P],
-                        rhs=vc[:].bitcast(FP8X4),
-                        rhs_scale=vs[:],
-                        start=True,
-                        stop=True,
-                    )
-                copy_on(O_COPY[pair], o_sb[:, 2 * pair : 2 * pair + 2, :], o_ps[:])
-            nc.sync.dma_start(
-                out=out[b, hh].rearrange("(p j) d -> p (j d)", j=NT),
-                in_=o_sb[:].rearrange("p j d -> p (j d)"),
-            )
-
-        prep_qk(0)
-        for h in range(NH + 1):
-            if h + 1 < NH:
-                prep_qk(h + 1)
-            if h < NH:
-                prep_v(h)
-            for j in range(NT):
-                if h < NH:
-                    scores(h, j)
-                if h >= 1:
-                    transpose_p(h - 1, j)
-            if h >= 1:
-                finish(h - 1)
+            t = tile_at(s, L_MAX)
+            if t is not None:
+                row_max(t)
+            t = tile_at(s, L_EXP)
+            if t is not None:
+                exp(t)
+            t = tile_at(s, L_NORM)
+            if t is not None:
+                norm(t)
+            u = pair_at(s, L_QUANT)
+            if u is not None:
+                p_quant(u)
+            u = pair_at(s, L_PCOPY)
+            if u is not None:
+                p_copy(u)
+            u = pair_at(s, L_OCOPY)
+            if u is not None:
+                o_copy(u)
+            if h + 1 < NH and 1 <= j < 3:
+                qk_copy(h + 1, j - 1)
+            if h < NH and j == 1:
+                v_regroup(h)
+            if h < NH and j == 3:
+                v_quant(h)
+            t = tile_at(s, L_STORE)
+            if t is not None and t % NT == NT - 1:
+                store(t // NT)

@@ -19,15 +19,11 @@ NT = S // P
 NSTEP = NH * NT
 FLOPS = 2 * 2 * NH * S * S * D
 
-PE_BIAS = (0, 1, 2, 3)
-NORM_ENGINE = "g"
-VREG_ENGINE = "v"
-QK_COPY = ("s", "v")
-P_COPY = ("s", "s")
-O_COPY = ("v", "v")
-PINNED = True
-PREFETCH = 3
-L_MAX, L_EXP, L_NORM, L_PT, L_PCOPY, L_QUANT, L_MX, L_OCOPY, L_STORE = 1, 2, 3, 5, 6, 7, 8, 9, 10
+PREFETCH = 4
+O_ENGINE = "v"
+Q_ENGINE = "s"
+P_ENGINE = ("s", "s")
+L_MX = 11
 
 
 def tile_fake_sd_mha_model_pa_t_kernel(tc, mat1, mat2, mat3, bias, out):
@@ -40,20 +36,28 @@ def tile_fake_sd_mha_model_pa_t_kernel(tc, mat1, mat2, mat3, bias, out):
             nc.vector.tensor_copy(out=dst, in_=src)
 
     with ExitStack() as ctx:
-        if PINNED:
-            ctx.enter_context(tc.manual_schedule())
+        ctx.enter_context(tc.manual_schedule())
         const = ctx.enter_context(tc.tile_pool(name="const", bufs=1))
         raw = ctx.enter_context(tc.tile_pool(name="raw", bufs=PREFETCH + 2))
-        work = ctx.enter_context(tc.tile_pool(name="work", bufs=3))
+        work = ctx.enter_context(tc.tile_pool(name="work", bufs=4))
         small = ctx.enter_context(tc.tile_pool(name="small", bufs=8))
         psum = ctx.enter_context(tc.psum_pool(name="psum", bufs=2))
 
         q_raw, k_raw, v_raw = {}, {}, {}
         tp_now, qT, kT, vg_now, v_q = {}, {}, {}, {}, {}
-        s_now, z_now, nm_now, e_now, sum_now, p_now = {}, {}, {}, {}, {}, {}
-        pt_now, g_now, pq_now, ops_now, osb_now = {}, {}, {}, {}, {}
+        s_now, nm_now, e_now, sum_now, p_now = {}, {}, {}, {}, {}
+        pt_now, g_now, pq_now, ops_now = {}, {}, {}, {}
+        bt_now = {}
 
-        def load(h):
+        bias_rows = bias[0, 0].rearrange("(p j) k -> p j k", j=NT)
+        bias_raw = const.tile([P, NT, S], BF16, name="bias_raw")
+        bias_perm = const.tile([P, NT, NT, P], BF16, name="bias_perm")
+        bias_t = const.tile([P, NT, NT, P], F32, name="bias_t")
+        ident_f = const.tile([P, P], F32, name="ident_f")
+        ident_b = const.tile([P, P], BF16, name="ident_b")
+        warm = const.tile([P, 1], F32, name="warm")
+
+        def load_qk(h):
             b, hh = divmod(h, NHB)
             q_raw[h] = raw.tile([P, NT * D], BF16, name="qr", tag="qr")
             nc.sync.dma_start(out=q_raw[h][:], in_=mat1[b, hh].rearrange("(p j) d -> p (j d)", j=NT))
@@ -68,27 +72,45 @@ def tile_fake_sd_mha_model_pa_t_kernel(tc, mat1, mat2, mat3, bias, out):
                 in_=mat3[b, hh].rearrange("(p t) d -> p (t d)", t=NT),
             )
 
+        def bias_permute(j):
+            nc.vector.tensor_copy(
+                out=bias_perm[:, j], in_=bias_raw[:, j, :].rearrange("p (c t) -> p t c", t=NT)
+            )
+
+        def bias_transpose(j):
+            bt_ps = psum.tile([P, 2, NT, P], BF16, name="bt_ps", tag="pt")
+            for t in range(NT):
+                nc.tensor.transpose(bt_ps[:, 0, t, :], bias_perm[:, j, t, :], ident_b[:])
+            bt_now[j] = bt_ps
+
+        def bias_keep(j):
+            nc.vector.tensor_copy(out=bias_t[:, j], in_=bt_now[j][:, 0])
+
         def qk_transpose(h, which):
-            src = (q_raw, k_raw)[which][h]
-            words = src[:].bitcast(F32)
-            tp = psum.tile([P, S], F32, name="tp", tag="tp")
+            words = (q_raw, k_raw)[which][h][:].bitcast(F32)
+            tp = psum.tile([P, S], F32, name="tp", tag="tp", bufs=1)
             for j in range(NT):
                 nc.tensor.transpose(tp[:, j * P : (j + 1) * P], words[:, j * P : (j + 1) * P], ident_f[:])
             tp_now[(h, which)] = tp
 
-        def qk_copy(h, which):
-            xt = work.tile([P, S], F32, name="xt", tag="xt%d" % which)
-            copy_on(QK_COPY[which], xt[:], tp_now[(h, which)][:])
-            (qT, kT)[which][h] = xt[:].bitcast(BF16).rearrange("w (c e) -> w c e", e=2)
+        def q_copy(h):
+            xt = work.tile([P, S], F32, name="xq", tag="xq")
+            copy_on(Q_ENGINE, xt[:], tp_now[(h, 0)][:])
+            qT[h] = xt[:].bitcast(BF16).rearrange("w (c e) -> w c e", e=2)
+
+        def k_copy(h):
+            xt = work.tile([P, S], F32, name="xk", tag="xk")
+            nc.vector.tensor_scalar_mul(
+                out=xt[:].bitcast(BF16), in0=tp_now[(h, 1)][:].bitcast(BF16), scalar1=1.0 / 16.0
+            )
+            kT[h] = xt[:].bitcast(BF16).rearrange("w (c e) -> w c e", e=2)
 
         def v_regroup(h):
             vg = work.tile([P, D, NT], BF16, name="vg", tag="vg", align_bytes=64)
-            dst = vg[:].rearrange("p (c i) t -> p c t i", i=4)
-            src = v_raw[h][:].rearrange("p t (c i) -> p c t i", i=4)
-            if VREG_ENGINE == "g":
-                nc.gpsimd.tensor_scalar(out=dst, in0=src, scalar1=1.0, scalar2=0.0, op0=ALU.mult, op1=ALU.add)
-            else:
-                nc.vector.tensor_copy(out=dst, in_=src)
+            nc.vector.tensor_copy(
+                out=vg[:].rearrange("p (c i) t -> p c t i", i=4),
+                in_=v_raw[h][:].rearrange("p t (c i) -> p c t i", i=4),
+            )
             vg_now[h] = vg
 
         def v_quant(h):
@@ -102,76 +124,57 @@ def tile_fake_sd_mha_model_pa_t_kernel(tc, mat1, mat2, mat3, bias, out):
         def mm(s, e):
             h, j = divmod(s, NT)
             if e == 0:
-                s_now[s] = psum.tile([P, S], F32, name="s_ps", tag="s", bufs=3)
+                s_now[s] = psum.tile([P, S], F32, name="s_ps", tag="s", bufs=4)
             nc.tensor.matmul(
                 s_now[s][:],
                 lhsT=qT[h][:, j * P : (j + 1) * P, e],
                 rhs=kT[h][:, :, e],
                 start=(e == 0),
-                stop=(e == 1 and j not in PE_BIAS),
+                stop=False,
             )
 
         def bias_add(s):
             j = s % NT
-            if j in PE_BIAS:
-                for t in range(NT):
-                    nc.tensor.matmul(
-                        s_now[s][:, t * P : (t + 1) * P],
-                        lhsT=bias_t[:, j, t, :],
-                        rhs=ident_f[:],
-                        is_transpose=True,
-                        start=False,
-                        stop=(t == NT - 1),
-                    )
+            for t in range(NT):
+                nc.tensor.matmul(
+                    s_now[s][:, t * P : (t + 1) * P],
+                    lhsT=bias_t[:, j, t, :],
+                    rhs=ident_f[:],
+                    is_transpose=True,
+                    start=False,
+                    stop=(t == NT - 1),
+                )
 
         def row_max(s):
-            j = s % NT
-            z = work.tile([P, S], F32, name="z", tag="z")
             nm = small.tile([P, 1], F32, name="nm", tag="nm")
-            if j in PE_BIAS:
-                nc.vector.tensor_scalar(
-                    out=z[:], in0=s_now[s][:], scalar1=-1.0 / 16.0, scalar2=None, op0=ALU.mult, op1=ALU.min,
-                    accum_out=nm[:],
-                )
-            else:
-                nc.vector.scalar_tensor_tensor(
-                    out=z[:],
-                    in0=s_now[s][:],
-                    scalar=1.0 / 16.0,
-                    in1=bias_perm[:, j].rearrange("p t c -> p (t c)"),
-                    op0=ALU.mult,
-                    op1=ALU.add,
-                )
-                nc.vector.tensor_reduce(out=nm[:], in_=z[:], axis=AX.X, op=ALU.max, negate=True)
-            z_now[s] = z
+            nc.vector.tensor_reduce(out=nm[:], in_=s_now[s][:], axis=AX.X, op=ALU.max, negate=True)
             nm_now[s] = nm
 
         def exp(s):
-            j = s % NT
-            e_sb = work.tile([P, S], F32, name="e_sb", tag="e")
-            ssum = small.tile([P, 1], F32, name="ssum", tag="ssum")
+            u, a = divmod(s, 2)
+            e_sb = work.tile([P, S], F32, name="e_sb", tag="e", bufs=6)
+            if a == 0:
+                sum_now[u] = small.tile([P, 2], F32, name="ssum", tag="ssum")
             nc.scalar.activation(
                 out=e_sb[:],
-                in_=z_now[s][:],
+                in_=s_now[s][:],
                 func=ACT.Exp,
                 bias=nm_now[s][:],
-                scale=(-1.0 if j in PE_BIAS else 1.0),
-                accum_out=ssum[:],
+                scale=1.0,
+                accum_out=sum_now[u][:, a : a + 1],
             )
             e_now[s] = e_sb
-            sum_now[s] = ssum
 
-        def norm(s):
-            r = small.tile([P, 1], F32, name="r", tag="r")
-            nc.vector.reciprocal(r[:], sum_now[s][:])
-            p_sb = work.tile([P, S], BF16, name="p_sb", tag="p", bufs=5)
-            if NORM_ENGINE == "g":
+        def norm(u):
+            r = small.tile([P, 2], F32, name="r", tag="r")
+            nc.vector.reciprocal(r[:], sum_now[u][:])
+            for a in range(2):
+                p_sb = work.tile([P, S], BF16, name="p_sb", tag="p", bufs=6)
                 nc.gpsimd.tensor_scalar(
-                    out=p_sb[:], in0=e_now[s][:], scalar1=r[:], scalar2=0.0, op0=ALU.mult, op1=ALU.add
+                    out=p_sb[:], in0=e_now[2 * u + a][:], scalar1=r[:, a : a + 1], scalar2=0.0,
+                    op0=ALU.mult, op1=ALU.add,
                 )
-            else:
-                nc.vector.tensor_scalar_mul(out=p_sb[:], in0=e_now[s][:], scalar1=r[:])
-            p_now[s] = p_sb
+                p_now[2 * u + a] = p_sb
 
         def p_transpose(s):
             u, a = divmod(s, 2)
@@ -182,7 +185,7 @@ def tile_fake_sd_mha_model_pa_t_kernel(tc, mat1, mat2, mat3, bias, out):
 
         def p_copy(u):
             g = work.tile([P, 2, P, NT], BF16, name="g", tag="g", align_bytes=64)
-            copy_on(P_COPY[u % 2], g[:], pt_now[u][:].rearrange("p a t q -> p a q t"))
+            copy_on(P_ENGINE[u % 2], g[:], pt_now[u][:].rearrange("p a t q -> p a q t"))
             g_now[u] = g
 
         def p_quant(u):
@@ -209,53 +212,14 @@ def tile_fake_sd_mha_model_pa_t_kernel(tc, mat1, mat2, mat3, bias, out):
                 )
             ops_now[u] = o_ps
 
-        def o_copy(u):
+        def o_copy_store(u):
             h, pair = divmod(u, 2)
-            if pair == 0:
-                osb_now[h] = work.tile([P, NT, D], F32, name="o_sb", tag="o")
-            copy_on(O_COPY[pair], osb_now[h][:, 2 * pair : 2 * pair + 2, :], ops_now[u][:])
-
-        def store(h):
             b, hh = divmod(h, NHB)
+            o_sb = work.tile([P, 2, D], F32, name="o_sb", tag="o")
+            copy_on(O_ENGINE, o_sb[:], ops_now[u][:])
             nc.sync.dma_start(
-                out=out[b, hh].rearrange("(p j) d -> p (j d)", j=NT),
-                in_=osb_now[h][:].rearrange("p j d -> p (j d)"),
+                out=out[b, hh].rearrange("(p j) d -> p j d", j=NT)[:, 2 * pair : 2 * pair + 2, :], in_=o_sb[:]
             )
-
-        load(0)
-        bias_raw = const.tile([P, NT, S], BF16, name="bias_raw")
-        nc.sync.dma_start(
-            out=bias_raw[:].rearrange("p j k -> p (j k)"), in_=bias[0, 0].rearrange("(p j) k -> p (j k)", j=NT)
-        )
-        load_v(0)
-        for h in range(1, PREFETCH):
-            load(h)
-            load_v(h)
-
-        ident_f = const.tile([P, P], F32, name="ident_f")
-        make_identity(nc, ident_f[:])
-        ident_b = const.tile([P, P], BF16, name="ident_b")
-        make_identity(nc, ident_b[:])
-        warm = const.tile([P, 1], F32, name="warm")
-        nc.vector.memset(warm[:], 0.0)
-        nc.scalar.activation(out=warm[:], in_=warm[:], func=ACT.Exp)
-
-        qk_transpose(0, 0)
-        qk_transpose(0, 1)
-        qk_copy(0, 0)
-        qk_copy(0, 1)
-
-        bias_perm = const.tile([P, NT, NT, P], BF16, name="bias_perm")
-        bias_t = const.tile([P, NT, NT, P], F32, name="bias_t")
-        for j in range(NT):
-            nc.vector.tensor_copy(
-                out=bias_perm[:, j], in_=bias_raw[:, j, :].rearrange("p (c t) -> p t c", t=NT)
-            )
-            if j in PE_BIAS:
-                bt_ps = psum.tile([P, 2, NT, P], BF16, name="bt_ps", tag="pt")
-                for t in range(NT):
-                    nc.tensor.transpose(bt_ps[:, 0, t, :], bias_perm[:, j, t, :], ident_b[:])
-                nc.vector.tensor_scalar_mul(out=bias_t[:, j], in0=bt_ps[:, 0], scalar1=16.0)
 
         def tile_at(s, lag):
             return s - lag if 0 <= s - lag < NSTEP else None
@@ -264,50 +228,90 @@ def tile_fake_sd_mha_model_pa_t_kernel(tc, mat1, mat2, mat3, bias, out):
             t = tile_at(s, lag)
             return t // 2 if t is not None and t % 2 == 1 else None
 
-        for s in range(NSTEP + L_STORE + 1):
-            h, j = divmod(s, NT)
-            if j == 0 and h + PREFETCH < NH:
-                load(h + PREFETCH)
+        def head_at(s, lead):
+            h, j = divmod(s + lead, NT)
+            return h if j == 0 and 0 <= h < NH else None
+
+        nc.sync.dma_start(out=bias_raw[:, 0, :], in_=bias_rows[:, 0, :])
+        load_qk(0)
+        nc.sync.dma_start(out=bias_raw[:, 1:NT, :], in_=bias_rows[:, 1:NT, :])
+        load_qk(1)
+        load_v(0)
+        load_v(1)
+        for h in range(2, PREFETCH):
+            load_qk(h)
+            load_v(h)
+        make_identity(nc, ident_b[:])
+        make_identity(nc, ident_f[:])
+        nc.vector.memset(warm[:], 0.0)
+        nc.scalar.activation(out=warm[:], in_=warm[:], func=ACT.Exp)
+        bias_permute(0)
+        bias_transpose(0)
+        bias_keep(0)
+
+        for s in range(-5, NSTEP + L_MX + 2):
+            h = head_at(s, 0)
+            if h is not None and h + PREFETCH < NH:
+                load_qk(h + PREFETCH)
                 load_v(h + PREFETCH)
+
             u_mx = pair_at(s, L_MX)
-            if s < NSTEP:
+            t_pt = tile_at(s, 6)
+            live = 0 <= s < NSTEP
+            if live:
                 mm(s, 0)
             if u_mx is not None:
                 mx(u_mx)
-            if s < NSTEP:
+            elif t_pt is not None:
+                p_transpose(t_pt)
+            if live:
                 mm(s, 1)
-            t = tile_at(s, L_PT)
-            if t is not None:
-                p_transpose(t)
-            if s < NSTEP:
+            if u_mx is not None and t_pt is not None:
+                p_transpose(t_pt)
+            h = head_at(s, 5)
+            if h is not None:
+                qk_transpose(h, 0)
+            h = head_at(s, 3)
+            if h is not None:
+                qk_transpose(h, 1)
+            if live:
                 bias_add(s)
-            if h + 1 < NH and j < 2:
-                qk_transpose(h + 1, j)
+            if 0 <= s < NT - 1:
+                bias_transpose(s + 1)
 
-            t = tile_at(s, L_MAX)
-            if t is not None:
-                row_max(t)
-            t = tile_at(s, L_EXP)
+            t = tile_at(s, 2)
             if t is not None:
                 exp(t)
-            t = tile_at(s, L_NORM)
-            if t is not None:
-                norm(t)
-            u = pair_at(s, L_QUANT)
-            if u is not None:
-                p_quant(u)
-            u = pair_at(s, L_PCOPY)
+            u = pair_at(s, 7)
             if u is not None:
                 p_copy(u)
-            u = pair_at(s, L_OCOPY)
+            h = head_at(s, 4)
+            if h is not None:
+                q_copy(h)
+
+            u = pair_at(s, 3)
             if u is not None:
-                o_copy(u)
-            if h + 1 < NH and 1 <= j < 3:
-                qk_copy(h + 1, j - 1)
-            if h < NH and j == 1:
+                norm(u)
+            t = tile_at(s, 1)
+            if t is not None:
+                row_max(t)
+            h = head_at(s, 2)
+            if h is not None:
+                k_copy(h)
+            if s == -1:
+                for j in range(1, NT):
+                    bias_permute(j)
+            if 0 <= s < NT - 1:
+                bias_keep(s + 1)
+            u = pair_at(s, L_MX + 1)
+            if u is not None:
+                o_copy_store(u)
+            u = pair_at(s, 8)
+            if u is not None:
+                p_quant(u)
+            h = head_at(s, -1)
+            if h is not None:
                 v_regroup(h)
-            if h < NH and j == 3:
+            h = head_at(s, -3)
+            if h is not None:
                 v_quant(h)
-            t = tile_at(s, L_STORE)
-            if t is not None and t % NT == NT - 1:
-                store(t // NT)

@@ -20,7 +20,7 @@ NSTEP = NH * NT
 FLOPS = 2 * 2 * NH * S * S * D
 
 PREFETCH = 4
-O_ENGINE = "v"
+O_ENGINE = ("v", "s")
 Q_ENGINE = "s"
 P_ENGINE = ("s", "s")
 L_MX = 11
@@ -216,7 +216,7 @@ def tile_fake_sd_mha_model_pa_t_kernel(tc, mat1, mat2, mat3, bias, out):
             h, pair = divmod(u, 2)
             b, hh = divmod(h, NHB)
             o_sb = work.tile([P, 2, D], F32, name="o_sb", tag="o")
-            copy_on(O_ENGINE, o_sb[:], ops_now[u][:])
+            copy_on(O_ENGINE[pair], o_sb[:], ops_now[u][:])
             nc.sync.dma_start(
                 out=out[b, hh].rearrange("(p j) d -> p j d", j=NT)[:, 2 * pair : 2 * pair + 2, :], in_=o_sb[:]
             )

@@ -124,7 +124,7 @@ def tile_fake_sd_mha_model_pa_t_kernel(tc, mat1, mat2, mat3, bias, out):
         def mm(s, e):
             h, j = divmod(s, NT)
             if e == 0:
-                s_now[s] = psum.tile([P, S], F32, name="s_ps", tag="s", bufs=4)
+                s_now[s] = psum.tile([P, S], F32, name="s_ps", tag="s", bufs=3)
             nc.tensor.matmul(
                 s_now[s][:],
                 lhsT=qT[h][:, j * P : (j + 1) * P, e],
@@ -199,7 +199,7 @@ def tile_fake_sd_mha_model_pa_t_kernel(tc, mat1, mat2, mat3, bias, out):
         def mx(u):
             pc, ps = pq_now[u]
             vc, vs = v_q[u // 2]
-            o_ps = psum.tile([P, 2, D], F32, name="o_ps", tag="o", bufs=1)
+            o_ps = psum.tile([P, 2, D], F32, name="o_ps", tag="o", bufs=2)
             for a in range(2):
                 nc.tensor.matmul_mx(
                     out=o_ps[:, a, :],

@@ -24,6 +24,7 @@ O_ENGINE = ("v", "s")
 Q_ENGINE = "s"
 P_ENGINE = ("s", "s")
 L_MX = 11
+VEC_BIAS = (3,)
 
 
 def tile_fake_sd_mha_model_pa_t_kernel(tc, mat1, mat2, mat3, bias, out):
@@ -57,10 +58,13 @@ def tile_fake_sd_mha_model_pa_t_kernel(tc, mat1, mat2, mat3, bias, out):
         ident_b = const.tile([P, P], BF16, name="ident_b")
         warm = const.tile([P, 1], F32, name="warm")
 
-        def load_qk(h):
+        def load_q(h):
             b, hh = divmod(h, NHB)
             q_raw[h] = raw.tile([P, NT * D], BF16, name="qr", tag="qr")
             nc.sync.dma_start(out=q_raw[h][:], in_=mat1[b, hh].rearrange("(p j) d -> p (j d)", j=NT))
+
+        def load_k(h):
+            b, hh = divmod(h, NHB)
             k_raw[h] = raw.tile([P, NT * D], BF16, name="kr", tag="kr")
             nc.sync.dma_start(out=k_raw[h][:], in_=mat2[b, hh].rearrange("(p j) d -> p (j d)", j=NT))
 
@@ -130,12 +134,12 @@ def tile_fake_sd_mha_model_pa_t_kernel(tc, mat1, mat2, mat3, bias, out):
                 lhsT=qT[h][:, j * P : (j + 1) * P, e],
                 rhs=kT[h][:, :, e],
                 start=(e == 0),
-                stop=False,
+                stop=(e == 1 and j in VEC_BIAS),
             )
 
         def bias_add(s):
             j = s % NT
-            for t in range(NT):
+            for t in range(NT if j not in VEC_BIAS else 0):
                 nc.tensor.matmul(
                     s_now[s][:, t * P : (t + 1) * P],
                     lhsT=bias_t[:, j, t, :],
@@ -146,7 +150,14 @@ def tile_fake_sd_mha_model_pa_t_kernel(tc, mat1, mat2, mat3, bias, out):
                 )
 
         def row_max(s):
+            j = s % NT
             nm = small.tile([P, 1], F32, name="nm", tag="nm")
+            if j in VEC_BIAS:
+                z = work.tile([P, S], F32, name="z", tag="z")
+                nc.vector.tensor_tensor(
+                    out=z[:], in0=s_now[s][:], in1=bias_perm[:, j].rearrange("p t c -> p (t c)"), op=ALU.add
+                )
+                s_now[s] = z
             nc.vector.tensor_reduce(out=nm[:], in_=s_now[s][:], axis=AX.X, op=ALU.max, negate=True)
             nm_now[s] = nm
 
@@ -233,13 +244,16 @@ def tile_fake_sd_mha_model_pa_t_kernel(tc, mat1, mat2, mat3, bias, out):
             return h if j == 0 and 0 <= h < NH else None
 
         nc.sync.dma_start(out=bias_raw[:, 0, :], in_=bias_rows[:, 0, :])
-        load_qk(0)
+        load_q(0)
+        load_k(0)
+        load_q(1)
         nc.sync.dma_start(out=bias_raw[:, 1:NT, :], in_=bias_rows[:, 1:NT, :])
-        load_qk(1)
+        load_k(1)
         load_v(0)
         load_v(1)
         for h in range(2, PREFETCH):
-            load_qk(h)
+            load_q(h)
+            load_k(h)
             load_v(h)
         make_identity(nc, ident_b[:])
         make_identity(nc, ident_f[:])
@@ -252,7 +266,8 @@ def tile_fake_sd_mha_model_pa_t_kernel(tc, mat1, mat2, mat3, bias, out):
         for s in range(-5, NSTEP + L_MX + 2):
             h = head_at(s, 0)
             if h is not None and h + PREFETCH < NH:
-                load_qk(h + PREFETCH)
+                load_q(h + PREFETCH)
+                load_k(h + PREFETCH)
                 load_v(h + PREFETCH)
 
             u_mx = pair_at(s, L_MX)
@@ -276,7 +291,7 @@ def tile_fake_sd_mha_model_pa_t_kernel(tc, mat1, mat2, mat3, bias, out):
                 qk_transpose(h, 1)
             if live:
                 bias_add(s)
-            if 0 <= s < NT - 1:
+            if 0 <= s < NT - 1 and s + 1 not in VEC_BIAS:
                 bias_transpose(s + 1)
 
             t = tile_at(s, 2)
@@ -298,10 +313,9 @@ def tile_fake_sd_mha_model_pa_t_kernel(tc, mat1, mat2, mat3, bias, out):
             h = head_at(s, 2)
             if h is not None:
                 k_copy(h)
-            if s == -1:
-                for j in range(1, NT):
-                    bias_permute(j)
-            if 0 <= s < NT - 1:
+            if 1 <= s + 2 < NT:
+                bias_permute(s + 2)
+            if 0 <= s < NT - 1 and s + 1 not in VEC_BIAS:
                 bias_keep(s + 1)
             u = pair_at(s, L_MX + 1)
             if u is not None:
@@ -309,9 +323,9 @@ def tile_fake_sd_mha_model_pa_t_kernel(tc, mat1, mat2, mat3, bias, out):
             u = pair_at(s, 8)
             if u is not None:
                 p_quant(u)
-            h = head_at(s, -1)
-            if h is not None:
-                v_regroup(h)
-            h = head_at(s, -3)
+            h = head_at(s, -5)
             if h is not None:
                 v_quant(h)
+            h = head_at(s, -3)
+            if h is not None:
+                v_regroup(h)

@@ -13,319 +13,258 @@ ACT = mybir.ActivationFunctionType
 AX = mybir.AxisListType
 
 P = 128
-NB, NHB, S, D = 8, 2, 512, 256
-NH = NB * NHB
-NT = S // P
-NSTEP = NH * NT
-FLOPS = 2 * 2 * NH * S * S * D
+HEADS_PER_BATCH, S, D = 2, 512, 256
+HEADS = 16
+TILES = S // P
+STEPS = HEADS * TILES
+FLOPS = 2 * 2 * HEADS * S * S * D
 
-PREFETCH = 4
-O_ENGINE = ("v", "s")
-Q_ENGINE = "s"
-P_ENGINE = ("s", "s")
-L_MX = 11
-VEC_BIAS = (3,)
+LOAD_LEAD = 4 * TILES
+Q_TRANSPOSE_LEAD, Q_COPY_LEAD, K_TRANSPOSE_LEAD, K_COPY_LEAD = 5, 4, 3, 2
+V_REGROUP_LAG, V_QUANT_LAG = 3, 7
+MAX_LAG, EXP_LAG, P_TRANSPOSE_LAG = 1, 2, 6
+NORM_LAG, P_COPY_LAG, P_QUANT_LAG, MX_LAG, OUT_LAG = 3, 7, 8, 11, 12
 
 
 def tile_fake_sd_mha_model_pa_t_kernel(tc, mat1, mat2, mat3, bias, out):
     nc = tc.nc
 
-    def copy_on(engine, dst, src):
-        if engine == "s":
-            nc.scalar.copy(out=dst, in_=src)
-        else:
-            nc.vector.tensor_copy(out=dst, in_=src)
-
     with ExitStack() as ctx:
         ctx.enter_context(tc.manual_schedule())
         const = ctx.enter_context(tc.tile_pool(name="const", bufs=1))
-        raw = ctx.enter_context(tc.tile_pool(name="raw", bufs=PREFETCH + 2))
+        raw = ctx.enter_context(tc.tile_pool(name="raw", bufs=6))
         work = ctx.enter_context(tc.tile_pool(name="work", bufs=4))
+        long_work = ctx.enter_context(tc.tile_pool(name="long_work", bufs=6))
         small = ctx.enter_context(tc.tile_pool(name="small", bufs=8))
         psum = ctx.enter_context(tc.psum_pool(name="psum", bufs=2))
 
-        q_raw, k_raw, v_raw = {}, {}, {}
-        tp_now, qT, kT, vg_now, v_q = {}, {}, {}, {}, {}
-        s_now, nm_now, e_now, sum_now, p_now = {}, {}, {}, {}, {}
-        pt_now, g_now, pq_now, ops_now = {}, {}, {}, {}
-        bt_now = {}
+        ident_f32 = const.tile([P, P], F32, name="ident_f32")
+        ident_bf16 = const.tile([P, P], BF16, name="ident_bf16")
+        bias_rows = const.tile([P, TILES, S], BF16, name="bias_rows")
+        bias_t = const.tile([P, TILES, TILES, P], F32, name="bias_t")
+        table_warm_up = const.tile([P, 1], F32, name="table_warm_up")
 
-        bias_rows = bias[0, 0].rearrange("(p j) k -> p j k", j=NT)
-        bias_raw = const.tile([P, NT, S], BF16, name="bias_raw")
-        bias_perm = const.tile([P, NT, NT, P], BF16, name="bias_perm")
-        bias_t = const.tile([P, NT, NT, P], F32, name="bias_t")
-        ident_f = const.tile([P, P], F32, name="ident_f")
-        ident_b = const.tile([P, P], BF16, name="ident_b")
-        warm = const.tile([P, 1], F32, name="warm")
+        q_rows, k_rows, v_rows, qk_banks, q_t, k_t, v_grouped, v_mx = {}, {}, {}, {}, {}, {}, {}, {}
+        score_banks, neg_max, e_tiles, p_tiles = {}, {}, {}, {}
+        row_sums, p_t_banks, p_grouped, p_mx, out_banks = {}, {}, {}, {}, {}
 
-        def load_q(h):
-            b, hh = divmod(h, NHB)
-            q_raw[h] = raw.tile([P, NT * D], BF16, name="qr", tag="qr")
-            nc.sync.dma_start(out=q_raw[h][:], in_=mat1[b, hh].rearrange("(p j) d -> p (j d)", j=NT))
+        def rows_of(tensor, head):
+            return tensor[head // HEADS_PER_BATCH, head % HEADS_PER_BATCH].rearrange("(p j) d -> p (j d)", j=TILES)
 
-        def load_k(h):
-            b, hh = divmod(h, NHB)
-            k_raw[h] = raw.tile([P, NT * D], BF16, name="kr", tag="kr")
-            nc.sync.dma_start(out=k_raw[h][:], in_=mat2[b, hh].rearrange("(p j) d -> p (j d)", j=NT))
+        def load(tensor, rows_by_head, tag, head):
+            rows_by_head[head] = raw.tile([P, TILES * D], BF16, name=tag, tag=tag)
+            nc.sync.dma_start(out=rows_by_head[head][:], in_=rows_of(tensor, head))
 
-        def load_v(h):
-            b, hh = divmod(h, NHB)
-            v_raw[h] = raw.tile([P, NT, D], BF16, name="vr", tag="vr")
-            nc.sync.dma_start(
-                out=v_raw[h][:].rearrange("p t d -> p (t d)"),
-                in_=mat3[b, hh].rearrange("(p t) d -> p (t d)", t=NT),
-            )
+        def load_head(head):
+            load(mat1, q_rows, "q_rows", head)
+            load(mat2, k_rows, "k_rows", head)
+            load(mat3, v_rows, "v_rows", head)
 
-        def bias_permute(j):
-            nc.vector.tensor_copy(
-                out=bias_perm[:, j], in_=bias_raw[:, j, :].rearrange("p (c t) -> p t c", t=NT)
-            )
+        def transpose_words(rows_by_head, head):
+            words = rows_by_head[head][:].bitcast(F32)
+            bank = psum.tile([P, S], F32, name="qk_bank", tag="qk_bank", bufs=1)
+            for j in range(TILES):
+                nc.tensor.transpose(bank[:, j * P : (j + 1) * P], words[:, j * P : (j + 1) * P], ident_f32[:])
+            qk_banks[head] = bank
 
-        def bias_transpose(j):
-            bt_ps = psum.tile([P, 2, NT, P], BF16, name="bt_ps", tag="pt")
-            for t in range(NT):
-                nc.tensor.transpose(bt_ps[:, 0, t, :], bias_perm[:, j, t, :], ident_b[:])
-            bt_now[j] = bt_ps
+        def by_parity(words_tile):
+            return words_tile[:].bitcast(BF16).rearrange("w (r e) -> w r e", e=2)
 
-        def bias_keep(j):
-            nc.vector.tensor_copy(out=bias_t[:, j], in_=bt_now[j][:, 0])
+        def copy_q(head):
+            words_tile = work.tile([P, S], F32, name="q_t", tag="q_t")
+            nc.scalar.copy(out=words_tile[:], in_=qk_banks[head][:])
+            q_t[head] = by_parity(words_tile)
 
-        def qk_transpose(h, which):
-            words = (q_raw, k_raw)[which][h][:].bitcast(F32)
-            tp = psum.tile([P, S], F32, name="tp", tag="tp", bufs=1)
-            for j in range(NT):
-                nc.tensor.transpose(tp[:, j * P : (j + 1) * P], words[:, j * P : (j + 1) * P], ident_f[:])
-            tp_now[(h, which)] = tp
-
-        def q_copy(h):
-            xt = work.tile([P, S], F32, name="xq", tag="xq")
-            copy_on(Q_ENGINE, xt[:], tp_now[(h, 0)][:])
-            qT[h] = xt[:].bitcast(BF16).rearrange("w (c e) -> w c e", e=2)
-
-        def k_copy(h):
-            xt = work.tile([P, S], F32, name="xk", tag="xk")
+        def copy_k(head):
+            words_tile = work.tile([P, S], F32, name="k_t", tag="k_t")
             nc.vector.tensor_scalar_mul(
-                out=xt[:].bitcast(BF16), in0=tp_now[(h, 1)][:].bitcast(BF16), scalar1=1.0 / 16.0
+                out=words_tile[:].bitcast(BF16), in0=qk_banks[head][:].bitcast(BF16), scalar1=1.0 / 16.0
             )
-            kT[h] = xt[:].bitcast(BF16).rearrange("w (c e) -> w c e", e=2)
+            k_t[head] = by_parity(words_tile)
 
-        def v_regroup(h):
-            vg = work.tile([P, D, NT], BF16, name="vg", tag="vg", align_bytes=64)
+        def transpose_bias():
+            for half, copy in enumerate((nc.vector.tensor_copy, nc.scalar.copy)):
+                bank = psum.tile([P, 2, TILES, P], BF16, name="bias_bank", tag="p_t_bank")
+                for a in range(2):
+                    keys_by_t = bias_rows[:, 2 * half + a, :].rearrange("p (c t) -> p t c", t=TILES)
+                    for t in range(TILES):
+                        nc.tensor.transpose(bank[:, a, t, :], keys_by_t[:, t, :], ident_bf16[:])
+                copy(out=bias_t[:, 2 * half : 2 * half + 2], in_=bank[:])
+
+        def regroup_v(head):
+            grouped = work.tile([P, D, TILES], BF16, name="v_grouped", tag="v_grouped", align_bytes=64)
             nc.vector.tensor_copy(
-                out=vg[:].rearrange("p (c i) t -> p c t i", i=4),
-                in_=v_raw[h][:].rearrange("p t (c i) -> p c t i", i=4),
+                out=grouped[:].rearrange("p (c i) t -> p c t i", i=4),
+                in_=v_rows[head][:].rearrange("p (t c i) -> p c t i", t=TILES, i=4),
             )
-            vg_now[h] = vg
+            v_grouped[head] = grouped
 
-        def v_quant(h):
-            vc = work.tile([P, D], U32, name="vc", tag="vc", align_bytes=64)
-            vs = work.tile([P, D], U8, name="vs", tag="vs", align_bytes=64)
-            nc.vector.quantize_mx(
-                out=vc[:].bitcast(FP8X4), scales=vs[:], in_=vg_now[h][:].rearrange("p d t -> p (d t)")
-            )
-            v_q[h] = (vc, vs)
+        def quantise(grouped, columns, tag):
+            words = work.tile([P, columns], U32, name=tag + "_words", tag=tag + "_words", align_bytes=64)
+            scales = work.tile([P, columns], U8, name=tag + "_scales", tag=tag + "_scales", align_bytes=64)
+            nc.vector.quantize_mx(out=words[:].bitcast(FP8X4), scales=scales[:], in_=grouped)
+            return words, scales
 
-        def mm(s, e):
-            h, j = divmod(s, NT)
+        def quantise_v(head):
+            v_mx[head] = quantise(v_grouped[head][:].rearrange("p d t -> p (d t)"), D, "v")
+
+        def score_matmul(tile, e):
+            head, j = divmod(tile, TILES)
             if e == 0:
-                s_now[s] = psum.tile([P, S], F32, name="s_ps", tag="s", bufs=3)
+                score_banks[tile] = psum.tile([P, S], F32, name="score_bank", tag="score_bank", bufs=3)
             nc.tensor.matmul(
-                s_now[s][:],
-                lhsT=qT[h][:, j * P : (j + 1) * P, e],
-                rhs=kT[h][:, :, e],
+                score_banks[tile][:],
+                lhsT=q_t[head][:, j * P : (j + 1) * P, e],
+                rhs=k_t[head][:, :, e],
                 start=(e == 0),
-                stop=(e == 1 and j in VEC_BIAS),
+                stop=False,
             )
 
-        def bias_add(s):
-            j = s % NT
-            for t in range(NT if j not in VEC_BIAS else 0):
+        def add_bias(tile):
+            j = tile % TILES
+            for t in range(TILES):
                 nc.tensor.matmul(
-                    s_now[s][:, t * P : (t + 1) * P],
+                    score_banks[tile][:, t * P : (t + 1) * P],
                     lhsT=bias_t[:, j, t, :],
-                    rhs=ident_f[:],
+                    rhs=ident_f32[:],
                     is_transpose=True,
                     start=False,
-                    stop=(t == NT - 1),
+                    stop=(t == TILES - 1),
                 )
 
-        def row_max(s):
-            j = s % NT
-            nm = small.tile([P, 1], F32, name="nm", tag="nm")
-            if j in VEC_BIAS:
-                z = work.tile([P, S], F32, name="z", tag="z")
-                nc.vector.tensor_tensor(
-                    out=z[:], in0=s_now[s][:], in1=bias_perm[:, j].rearrange("p t c -> p (t c)"), op=ALU.add
-                )
-                s_now[s] = z
-            nc.vector.tensor_reduce(out=nm[:], in_=s_now[s][:], axis=AX.X, op=ALU.max, negate=True)
-            nm_now[s] = nm
+        def row_max(tile):
+            neg_max[tile] = small.tile([P, 1], F32, name="neg_max", tag="neg_max")
+            nc.vector.tensor_reduce(
+                out=neg_max[tile][:], in_=score_banks[tile][:], axis=AX.X, op=ALU.max, negate=True
+            )
 
-        def exp(s):
-            u, a = divmod(s, 2)
-            e_sb = work.tile([P, S], F32, name="e_sb", tag="e", bufs=6)
+        def exponential(tile):
+            pair, a = divmod(tile, 2)
             if a == 0:
-                sum_now[u] = small.tile([P, 2], F32, name="ssum", tag="ssum")
+                row_sums[pair] = small.tile([P, 2], F32, name="row_sums", tag="row_sums")
+            e_tiles[tile] = long_work.tile([P, S], F32, name="e_tile", tag="e_tile")
             nc.scalar.activation(
-                out=e_sb[:],
-                in_=s_now[s][:],
+                out=e_tiles[tile][:],
+                in_=score_banks[tile][:],
                 func=ACT.Exp,
-                bias=nm_now[s][:],
+                bias=neg_max[tile][:],
                 scale=1.0,
-                accum_out=sum_now[u][:, a : a + 1],
+                accum_out=row_sums[pair][:, a : a + 1],
             )
-            e_now[s] = e_sb
 
-        def norm(u):
-            r = small.tile([P, 2], F32, name="r", tag="r")
-            nc.vector.reciprocal(r[:], sum_now[u][:])
+        def normalise(pair):
+            inverse = small.tile([P, 2], F32, name="inverse", tag="inverse")
+            nc.vector.reciprocal(inverse[:], row_sums[pair][:])
             for a in range(2):
-                p_sb = work.tile([P, S], BF16, name="p_sb", tag="p", bufs=6)
+                tile = 2 * pair + a
+                p_tiles[tile] = long_work.tile([P, S], BF16, name="p_tile", tag="p_tile")
                 nc.gpsimd.tensor_scalar(
-                    out=p_sb[:], in0=e_now[2 * u + a][:], scalar1=r[:, a : a + 1], scalar2=0.0,
-                    op0=ALU.mult, op1=ALU.add,
+                    out=p_tiles[tile][:],
+                    in0=e_tiles[tile][:],
+                    scalar1=inverse[:, a : a + 1],
+                    scalar2=0.0,
+                    op0=ALU.mult,
+                    op1=ALU.add,
                 )
-                p_now[2 * u + a] = p_sb
 
-        def p_transpose(s):
-            u, a = divmod(s, 2)
+        def transpose_p(tile):
+            pair, a = divmod(tile, 2)
             if a == 0:
-                pt_now[u] = psum.tile([P, 2, NT, P], BF16, name="pt_ps", tag="pt")
-            for t in range(NT):
-                nc.tensor.transpose(pt_now[u][:, a, t, :], p_now[s][:, t * P : (t + 1) * P], ident_b[:])
+                p_t_banks[pair] = psum.tile([P, 2, TILES, P], BF16, name="p_t_bank", tag="p_t_bank")
+            for t in range(TILES):
+                nc.tensor.transpose(
+                    p_t_banks[pair][:, a, t, :], p_tiles[tile][:, t * P : (t + 1) * P], ident_bf16[:]
+                )
 
-        def p_copy(u):
-            g = work.tile([P, 2, P, NT], BF16, name="g", tag="g", align_bytes=64)
-            copy_on(P_ENGINE[u % 2], g[:], pt_now[u][:].rearrange("p a t q -> p a q t"))
-            g_now[u] = g
+        def copy_p(pair):
+            p_grouped[pair] = work.tile([P, 2, P, TILES], BF16, name="p_grouped", tag="p_grouped", align_bytes=64)
+            nc.scalar.copy(out=p_grouped[pair][:], in_=p_t_banks[pair][:].rearrange("c a t q -> c a q t"))
 
-        def p_quant(u):
-            pc = work.tile([P, 2 * P], U32, name="pc", tag="pc", align_bytes=64)
-            ps = work.tile([P, 2 * P], U8, name="ps", tag="ps", align_bytes=64)
-            nc.vector.quantize_mx(
-                out=pc[:].bitcast(FP8X4), scales=ps[:], in_=g_now[u][:].rearrange("p a q t -> p (a q t)")
-            )
-            pq_now[u] = (pc, ps)
+        def quantise_p(pair):
+            p_mx[pair] = quantise(p_grouped[pair][:].rearrange("c a q t -> c (a q t)"), 2 * P, "p")
 
-        def mx(u):
-            pc, ps = pq_now[u]
-            vc, vs = v_q[u // 2]
-            o_ps = psum.tile([P, 2, D], F32, name="o_ps", tag="o", bufs=2)
+        def mx_passes(pair):
+            p_words, p_scales = p_mx[pair]
+            v_words, v_scales = v_mx[pair // 2]
+            out_banks[pair] = psum.tile([P, 2, D], F32, name="out_bank", tag="out_bank")
             for a in range(2):
                 nc.tensor.matmul_mx(
-                    out=o_ps[:, a, :],
-                    lhsT=pc[:, a * P : (a + 1) * P].bitcast(FP8X4),
-                    lhsT_scale=ps[:, a * P : (a + 1) * P],
-                    rhs=vc[:].bitcast(FP8X4),
-                    rhs_scale=vs[:],
+                    out=out_banks[pair][:, a, :],
+                    lhsT=p_words[:, a * P : (a + 1) * P].bitcast(FP8X4),
+                    lhsT_scale=p_scales[:, a * P : (a + 1) * P],
+                    rhs=v_words[:].bitcast(FP8X4),
+                    rhs_scale=v_scales[:],
                     start=True,
                     stop=True,
                 )
-            ops_now[u] = o_ps
 
-        def o_copy_store(u):
-            h, pair = divmod(u, 2)
-            b, hh = divmod(h, NHB)
-            o_sb = work.tile([P, 2, D], F32, name="o_sb", tag="o")
-            copy_on(O_ENGINE[pair], o_sb[:], ops_now[u][:])
-            nc.sync.dma_start(
-                out=out[b, hh].rearrange("(p j) d -> p j d", j=NT)[:, 2 * pair : 2 * pair + 2, :], in_=o_sb[:]
-            )
+        def store(pair):
+            head, half = divmod(pair, 2)
+            result = work.tile([P, 2 * D], F32, name="result", tag="result")
+            copy = (nc.vector.tensor_copy, nc.scalar.copy)[half]
+            copy(out=result[:], in_=out_banks[pair][:].rearrange("p a d -> p (a d)"))
+            nc.sync.dma_start(out=rows_of(out, head)[:, half * 2 * D : (half + 1) * 2 * D], in_=result[:])
 
-        def tile_at(s, lag):
-            return s - lag if 0 <= s - lag < NSTEP else None
+        def tile_behind(step, lag):
+            return step - lag if 0 <= step - lag < STEPS else None
 
-        def pair_at(s, lag):
-            t = tile_at(s, lag)
-            return t // 2 if t is not None and t % 2 == 1 else None
+        def pair_behind(step, lag):
+            tile = tile_behind(step, lag)
+            return tile // 2 if tile is not None and tile % 2 == 1 else None
 
-        def head_at(s, lead):
-            h, j = divmod(s + lead, NT)
-            return h if j == 0 and 0 <= h < NH else None
+        def head_starting(step):
+            head, j = divmod(step, TILES)
+            return head if j == 0 and 0 <= head < HEADS else None
 
-        nc.sync.dma_start(out=bias_raw[:, 0, :], in_=bias_rows[:, 0, :])
-        load_q(0)
-        load_k(0)
-        load_q(1)
-        nc.sync.dma_start(out=bias_raw[:, 1:NT, :], in_=bias_rows[:, 1:NT, :])
-        load_k(1)
-        load_v(0)
-        load_v(1)
-        for h in range(2, PREFETCH):
-            load_q(h)
-            load_k(h)
-            load_v(h)
-        make_identity(nc, ident_b[:])
-        make_identity(nc, ident_f[:])
-        nc.vector.memset(warm[:], 0.0)
-        nc.scalar.activation(out=warm[:], in_=warm[:], func=ACT.Exp)
-        bias_permute(0)
-        bias_transpose(0)
-        bias_keep(0)
+        def run(stage, index):
+            if index is not None:
+                stage(index)
 
-        for s in range(-5, NSTEP + L_MX + 2):
-            h = head_at(s, 0)
-            if h is not None and h + PREFETCH < NH:
-                load_q(h + PREFETCH)
-                load_k(h + PREFETCH)
-                load_v(h + PREFETCH)
+        load(mat1, q_rows, "q_rows", 0)
+        load(mat2, k_rows, "k_rows", 0)
+        nc.sync.dma_start(
+            out=bias_rows[:].rearrange("p j k -> p (j k)"), in_=bias[0, 0].rearrange("(p j) k -> p (j k)", j=TILES)
+        )
+        load(mat1, q_rows, "q_rows", 1)
+        load(mat2, k_rows, "k_rows", 1)
+        load(mat3, v_rows, "v_rows", 0)
+        load(mat3, v_rows, "v_rows", 1)
+        for head in range(2, LOAD_LEAD // TILES):
+            load_head(head)
+        make_identity(nc, ident_f32[:])
+        make_identity(nc, ident_bf16[:])
+        nc.vector.memset(table_warm_up[:], 0.0)
+        nc.scalar.activation(out=table_warm_up[:], in_=table_warm_up[:], func=ACT.Exp)
+        transpose_words(q_rows, 0)
+        copy_q(0)
+        transpose_words(k_rows, 0)
+        copy_k(0)
+        transpose_bias()
 
-            u_mx = pair_at(s, L_MX)
-            t_pt = tile_at(s, 6)
-            live = 0 <= s < NSTEP
-            if live:
-                mm(s, 0)
-            if u_mx is not None:
-                mx(u_mx)
-            elif t_pt is not None:
-                p_transpose(t_pt)
-            if live:
-                mm(s, 1)
-            if u_mx is not None and t_pt is not None:
-                p_transpose(t_pt)
-            h = head_at(s, 5)
-            if h is not None:
-                qk_transpose(h, 0)
-            h = head_at(s, 3)
-            if h is not None:
-                qk_transpose(h, 1)
-            if live:
-                bias_add(s)
-            if 0 <= s < NT - 1 and s + 1 not in VEC_BIAS:
-                bias_transpose(s + 1)
+        for step in range(-1, STEPS + OUT_LAG + 1):
+            run(load_head, head_starting(step + LOAD_LEAD))
 
-            t = tile_at(s, 2)
-            if t is not None:
-                exp(t)
-            u = pair_at(s, 7)
-            if u is not None:
-                p_copy(u)
-            h = head_at(s, 4)
-            if h is not None:
-                q_copy(h)
+            scores_now = tile_behind(step, 0)
+            pair_for_mx = pair_behind(step, MX_LAG)
+            run(lambda tile: score_matmul(tile, 0), scores_now)
+            if pair_for_mx is None:
+                run(transpose_p, tile_behind(step, P_TRANSPOSE_LAG))
+            run(mx_passes, pair_for_mx)
+            run(lambda tile: score_matmul(tile, 1), scores_now)
+            if pair_for_mx is not None:
+                run(transpose_p, tile_behind(step, P_TRANSPOSE_LAG))
+            run(lambda head: transpose_words(q_rows, head), head_starting(step + Q_TRANSPOSE_LEAD))
+            run(lambda head: transpose_words(k_rows, head), head_starting(step + K_TRANSPOSE_LEAD))
+            run(add_bias, scores_now)
 
-            u = pair_at(s, 3)
-            if u is not None:
-                norm(u)
-            t = tile_at(s, 1)
-            if t is not None:
-                row_max(t)
-            h = head_at(s, 2)
-            if h is not None:
-                k_copy(h)
-            if 1 <= s + 2 < NT:
-                bias_permute(s + 2)
-            if 0 <= s < NT - 1 and s + 1 not in VEC_BIAS:
-                bias_keep(s + 1)
-            u = pair_at(s, L_MX + 1)
-            if u is not None:
-                o_copy_store(u)
-            u = pair_at(s, 8)
-            if u is not None:
-                p_quant(u)
-            h = head_at(s, -5)
-            if h is not None:
-                v_quant(h)
-            h = head_at(s, -3)
-            if h is not None:
-                v_regroup(h)
+            run(exponential, tile_behind(step, EXP_LAG))
+            run(copy_p, pair_behind(step, P_COPY_LAG))
+            run(copy_q, head_starting(step + Q_COPY_LEAD))
+
+            run(normalise, pair_behind(step, NORM_LAG))
+            run(row_max, tile_behind(step, MAX_LAG))
+            run(copy_k, head_starting(step + K_COPY_LEAD))
+            run(store, pair_behind(step, OUT_LAG))
+            run(quantise_p, pair_behind(step, P_QUANT_LAG))
+            run(quantise_v, head_starting(step - V_QUANT_LAG))
+            run(regroup_v, head_starting(step - V_REGROUP_LAG))

@@ -22,8 +22,8 @@ FLOPS = 2 * 2 * HEADS * S * S * D
 LOAD_LEAD = 4 * TILES
 Q_TRANSPOSE_LEAD, Q_COPY_LEAD, K_TRANSPOSE_LEAD, K_COPY_LEAD = 5, 4, 3, 2
 V_REGROUP_LAG, V_QUANT_LAG = 3, 7
-MAX_LAG, EXP_LAG, P_TRANSPOSE_LAG = 1, 2, 6
-NORM_LAG, P_COPY_LAG, P_QUANT_LAG, MX_LAG, OUT_LAG = 3, 7, 8, 11, 12
+MAX_LAG, EXP_LAG, PROB_TRANSPOSE_LAG = 1, 2, 6
+NORM_LAG, PROB_COPY_LAG, PROB_QUANT_LAG, MX_LAG, OUT_LAG = 3, 7, 8, 11, 12
 
 
 def tile_fake_sd_mha_model_pa_t_kernel(tc, mat1, mat2, mat3, bias, out):
@@ -45,8 +45,8 @@ def tile_fake_sd_mha_model_pa_t_kernel(tc, mat1, mat2, mat3, bias, out):
         table_warm_up = const.tile([P, 1], F32, name="table_warm_up")
 
         q_rows, k_rows, v_rows, qk_banks, q_t, k_t, v_grouped, v_mx = {}, {}, {}, {}, {}, {}, {}, {}
-        score_banks, neg_max, e_tiles, p_tiles = {}, {}, {}, {}
-        row_sums, p_t_banks, p_grouped, p_mx, out_banks = {}, {}, {}, {}, {}
+        score_banks, neg_max, e_values, prob_values = {}, {}, {}, {}
+        row_sums, prob_t_banks, prob_grouped, prob_mx, out_banks = {}, {}, {}, {}, {}
 
         def rows_of(tensor, head):
             return tensor[head // HEADS_PER_BATCH, head % HEADS_PER_BATCH].rearrange("(p j) d -> p (j d)", j=TILES)
@@ -67,64 +67,64 @@ def tile_fake_sd_mha_model_pa_t_kernel(tc, mat1, mat2, mat3, bias, out):
                 nc.tensor.transpose(bank[:, j * P : (j + 1) * P], words[:, j * P : (j + 1) * P], ident_f32[:])
             qk_banks[head] = bank
 
-        def by_parity(words_tile):
-            return words_tile[:].bitcast(BF16).rearrange("w (r e) -> w r e", e=2)
+        def by_parity(words):
+            return words[:].bitcast(BF16).rearrange("w (row parity) -> w row parity", parity=2)
 
         def copy_q(head):
-            words_tile = work.tile([P, S], F32, name="q_t", tag="q_t")
-            nc.scalar.copy(out=words_tile[:], in_=qk_banks[head][:])
-            q_t[head] = by_parity(words_tile)
+            words = work.tile([P, S], F32, name="q_t", tag="q_t")
+            nc.scalar.copy(out=words[:], in_=qk_banks[head][:])
+            q_t[head] = by_parity(words)
 
         def copy_k(head):
-            words_tile = work.tile([P, S], F32, name="k_t", tag="k_t")
+            words = work.tile([P, S], F32, name="k_t", tag="k_t")
             nc.vector.tensor_scalar_mul(
-                out=words_tile[:].bitcast(BF16), in0=qk_banks[head][:].bitcast(BF16), scalar1=1.0 / 16.0
+                out=words[:].bitcast(BF16), in0=qk_banks[head][:].bitcast(BF16), scalar1=1.0 / 16.0
             )
-            k_t[head] = by_parity(words_tile)
+            k_t[head] = by_parity(words)
 
         def transpose_bias():
-            for half, copy in enumerate((nc.vector.tensor_copy, nc.scalar.copy)):
-                bank = psum.tile([P, 2, TILES, P], BF16, name="bias_bank", tag="p_t_bank")
+            for pair, copy in enumerate((nc.vector.tensor_copy, nc.scalar.copy)):
+                bank = psum.tile([P, 2, TILES, P], BF16, name="bias_bank", tag="prob_t_bank")
                 for a in range(2):
-                    keys_by_t = bias_rows[:, 2 * half + a, :].rearrange("p (c t) -> p t c", t=TILES)
+                    keys_by_t = bias_rows[:, 2 * pair + a, :].rearrange("p (c t) -> p t c", t=TILES)
                     for t in range(TILES):
                         nc.tensor.transpose(bank[:, a, t, :], keys_by_t[:, t, :], ident_bf16[:])
-                copy(out=bias_t[:, 2 * half : 2 * half + 2], in_=bank[:])
+                copy(out=bias_t[:, 2 * pair : 2 * pair + 2], in_=bank[:])
 
         def regroup_v(head):
             grouped = work.tile([P, D, TILES], BF16, name="v_grouped", tag="v_grouped", align_bytes=64)
             nc.vector.tensor_copy(
-                out=grouped[:].rearrange("p (c i) t -> p c t i", i=4),
-                in_=v_rows[head][:].rearrange("p (t c i) -> p c t i", t=TILES, i=4),
+                out=grouped[:].rearrange("p (run i) t -> p run t i", i=4),
+                in_=v_rows[head][:].rearrange("p (t run i) -> p run t i", t=TILES, i=4),
             )
             v_grouped[head] = grouped
 
         def quantise(grouped, columns, tag):
-            words = work.tile([P, columns], U32, name=tag + "_words", tag=tag + "_words", align_bytes=64)
+            codes = work.tile([P, columns], U32, name=tag + "_codes", tag=tag + "_codes", align_bytes=64)
             scales = work.tile([P, columns], U8, name=tag + "_scales", tag=tag + "_scales", align_bytes=64)
-            nc.vector.quantize_mx(out=words[:].bitcast(FP8X4), scales=scales[:], in_=grouped)
-            return words, scales
+            nc.vector.quantize_mx(out=codes[:].bitcast(FP8X4), scales=scales[:], in_=grouped)
+            return codes, scales
 
         def quantise_v(head):
             v_mx[head] = quantise(v_grouped[head][:].rearrange("p d t -> p (d t)"), D, "v")
 
-        def score_matmul(tile, e):
-            head, j = divmod(tile, TILES)
-            if e == 0:
-                score_banks[tile] = psum.tile([P, S], F32, name="score_bank", tag="score_bank", bufs=3)
+        def score_matmul(q_tile, parity):
+            head, j = divmod(q_tile, TILES)
+            if parity == 0:
+                score_banks[q_tile] = psum.tile([P, S], F32, name="score_bank", tag="score_bank", bufs=3)
             nc.tensor.matmul(
-                score_banks[tile][:],
-                lhsT=q_t[head][:, j * P : (j + 1) * P, e],
-                rhs=k_t[head][:, :, e],
-                start=(e == 0),
+                score_banks[q_tile][:],
+                lhsT=q_t[head][:, j * P : (j + 1) * P, parity],
+                rhs=k_t[head][:, :, parity],
+                start=(parity == 0),
                 stop=False,
             )
 
-        def add_bias(tile):
-            j = tile % TILES
+        def add_bias(q_tile):
+            j = q_tile % TILES
             for t in range(TILES):
                 nc.tensor.matmul(
-                    score_banks[tile][:, t * P : (t + 1) * P],
+                    score_banks[q_tile][:, t * P : (t + 1) * P],
                     lhsT=bias_t[:, j, t, :],
                     rhs=ident_f32[:],
                     is_transpose=True,
@@ -132,22 +132,22 @@ def tile_fake_sd_mha_model_pa_t_kernel(tc, mat1, mat2, mat3, bias, out):
                     stop=(t == TILES - 1),
                 )
 
-        def row_max(tile):
-            neg_max[tile] = small.tile([P, 1], F32, name="neg_max", tag="neg_max")
+        def row_max(q_tile):
+            neg_max[q_tile] = small.tile([P, 1], F32, name="neg_max", tag="neg_max")
             nc.vector.tensor_reduce(
-                out=neg_max[tile][:], in_=score_banks[tile][:], axis=AX.X, op=ALU.max, negate=True
+                out=neg_max[q_tile][:], in_=score_banks[q_tile][:], axis=AX.X, op=ALU.max, negate=True
             )
 
-        def exponential(tile):
-            pair, a = divmod(tile, 2)
+        def exponential(q_tile):
+            pair, a = divmod(q_tile, 2)
             if a == 0:
                 row_sums[pair] = small.tile([P, 2], F32, name="row_sums", tag="row_sums")
-            e_tiles[tile] = long_work.tile([P, S], F32, name="e_tile", tag="e_tile")
+            e_values[q_tile] = long_work.tile([P, S], F32, name="e_values", tag="e_values")
             nc.scalar.activation(
-                out=e_tiles[tile][:],
-                in_=score_banks[tile][:],
+                out=e_values[q_tile][:],
+                in_=score_banks[q_tile][:],
                 func=ACT.Exp,
-                bias=neg_max[tile][:],
+                bias=neg_max[q_tile][:],
                 scale=1.0,
                 accum_out=row_sums[pair][:, a : a + 1],
             )
@@ -156,61 +156,64 @@ def tile_fake_sd_mha_model_pa_t_kernel(tc, mat1, mat2, mat3, bias, out):
             inverse = small.tile([P, 2], F32, name="inverse", tag="inverse")
             nc.vector.reciprocal(inverse[:], row_sums[pair][:])
             for a in range(2):
-                tile = 2 * pair + a
-                p_tiles[tile] = long_work.tile([P, S], BF16, name="p_tile", tag="p_tile")
+                q_tile = 2 * pair + a
+                prob_values[q_tile] = long_work.tile([P, S], BF16, name="prob_values", tag="prob_values")
                 nc.gpsimd.tensor_scalar(
-                    out=p_tiles[tile][:],
-                    in0=e_tiles[tile][:],
+                    out=prob_values[q_tile][:],
+                    in0=e_values[q_tile][:],
                     scalar1=inverse[:, a : a + 1],
                     scalar2=0.0,
                     op0=ALU.mult,
                     op1=ALU.add,
                 )
 
-        def transpose_p(tile):
-            pair, a = divmod(tile, 2)
+        def transpose_prob(q_tile):
+            pair, a = divmod(q_tile, 2)
             if a == 0:
-                p_t_banks[pair] = psum.tile([P, 2, TILES, P], BF16, name="p_t_bank", tag="p_t_bank")
+                prob_t_banks[pair] = psum.tile([P, 2, TILES, P], BF16, name="prob_t_bank", tag="prob_t_bank")
             for t in range(TILES):
                 nc.tensor.transpose(
-                    p_t_banks[pair][:, a, t, :], p_tiles[tile][:, t * P : (t + 1) * P], ident_bf16[:]
+                    prob_t_banks[pair][:, a, t, :], prob_values[q_tile][:, t * P : (t + 1) * P], ident_bf16[:]
                 )
 
-        def copy_p(pair):
-            p_grouped[pair] = work.tile([P, 2, P, TILES], BF16, name="p_grouped", tag="p_grouped", align_bytes=64)
-            nc.scalar.copy(out=p_grouped[pair][:], in_=p_t_banks[pair][:].rearrange("c a t q -> c a q t"))
+        def copy_prob(pair):
+            grouped = work.tile([P, 2, P, TILES], BF16, name="prob_grouped", tag="prob_grouped", align_bytes=64)
+            nc.scalar.copy(out=grouped[:], in_=prob_t_banks[pair][:].rearrange("c a t p -> c a p t"))
+            prob_grouped[pair] = grouped
 
-        def quantise_p(pair):
-            p_mx[pair] = quantise(p_grouped[pair][:].rearrange("c a q t -> c (a q t)"), 2 * P, "p")
+        def quantise_prob(pair):
+            prob_mx[pair] = quantise(prob_grouped[pair][:].rearrange("c a p t -> c (a p t)"), 2 * P, "prob")
 
         def mx_passes(pair):
-            p_words, p_scales = p_mx[pair]
-            v_words, v_scales = v_mx[pair // 2]
+            prob_codes, prob_scales = prob_mx[pair]
+            v_codes, v_scales = v_mx[pair // 2]
             out_banks[pair] = psum.tile([P, 2, D], F32, name="out_bank", tag="out_bank")
             for a in range(2):
                 nc.tensor.matmul_mx(
                     out=out_banks[pair][:, a, :],
-                    lhsT=p_words[:, a * P : (a + 1) * P].bitcast(FP8X4),
-                    lhsT_scale=p_scales[:, a * P : (a + 1) * P],
-                    rhs=v_words[:].bitcast(FP8X4),
+                    lhsT=prob_codes[:, a * P : (a + 1) * P].bitcast(FP8X4),
+                    lhsT_scale=prob_scales[:, a * P : (a + 1) * P],
+                    rhs=v_codes[:].bitcast(FP8X4),
                     rhs_scale=v_scales[:],
                     start=True,
                     stop=True,
                 )
 
         def store(pair):
-            head, half = divmod(pair, 2)
+            head, pair_of_head = divmod(pair, 2)
             result = work.tile([P, 2 * D], F32, name="result", tag="result")
-            copy = (nc.vector.tensor_copy, nc.scalar.copy)[half]
+            copy = (nc.vector.tensor_copy, nc.scalar.copy)[pair_of_head]
             copy(out=result[:], in_=out_banks[pair][:].rearrange("p a d -> p (a d)"))
-            nc.sync.dma_start(out=rows_of(out, head)[:, half * 2 * D : (half + 1) * 2 * D], in_=result[:])
+            nc.sync.dma_start(
+                out=rows_of(out, head)[:, pair_of_head * 2 * D : (pair_of_head + 1) * 2 * D], in_=result[:]
+            )
 
         def tile_behind(step, lag):
             return step - lag if 0 <= step - lag < STEPS else None
 
         def pair_behind(step, lag):
-            tile = tile_behind(step, lag)
-            return tile // 2 if tile is not None and tile % 2 == 1 else None
+            q_tile = tile_behind(step, lag)
+            return q_tile // 2 if q_tile is not None and q_tile % 2 == 1 else None
 
         def head_starting(step):
             head, j = divmod(step, TILES)
@@ -246,25 +249,25 @@ def tile_fake_sd_mha_model_pa_t_kernel(tc, mat1, mat2, mat3, bias, out):
 
             scores_now = tile_behind(step, 0)
             pair_for_mx = pair_behind(step, MX_LAG)
-            run(lambda tile: score_matmul(tile, 0), scores_now)
+            run(lambda q_tile: score_matmul(q_tile, 0), scores_now)
             if pair_for_mx is None:
-                run(transpose_p, tile_behind(step, P_TRANSPOSE_LAG))
+                run(transpose_prob, tile_behind(step, PROB_TRANSPOSE_LAG))
             run(mx_passes, pair_for_mx)
-            run(lambda tile: score_matmul(tile, 1), scores_now)
+            run(lambda q_tile: score_matmul(q_tile, 1), scores_now)
             if pair_for_mx is not None:
-                run(transpose_p, tile_behind(step, P_TRANSPOSE_LAG))
+                run(transpose_prob, tile_behind(step, PROB_TRANSPOSE_LAG))
             run(lambda head: transpose_words(q_rows, head), head_starting(step + Q_TRANSPOSE_LEAD))
             run(lambda head: transpose_words(k_rows, head), head_starting(step + K_TRANSPOSE_LEAD))
             run(add_bias, scores_now)
 
             run(exponential, tile_behind(step, EXP_LAG))
-            run(copy_p, pair_behind(step, P_COPY_LAG))
+            run(copy_prob, pair_behind(step, PROB_COPY_LAG))
             run(copy_q, head_starting(step + Q_COPY_LEAD))
 
             run(normalise, pair_behind(step, NORM_LAG))
             run(row_max, tile_behind(step, MAX_LAG))
             run(copy_k, head_starting(step + K_COPY_LEAD))
             run(store, pair_behind(step, OUT_LAG))
-            run(quantise_p, pair_behind(step, P_QUANT_LAG))
+            run(quantise_prob, pair_behind(step, PROB_QUANT_LAG))
             run(quantise_v, head_starting(step - V_QUANT_LAG))
             run(regroup_v, head_starting(step - V_REGROUP_LAG))

@@ -159,8 +159,8 @@ def tile_fake_sd_mha_model_pa_t_kernel(tc, mat1, mat2, mat3, bias, out):
                 q_tile = 2 * pair + a
                 prob_values[q_tile] = long_work.tile([P, S], BF16, name="prob_values", tag="prob_values")
                 nc.gpsimd.tensor_scalar(
-                    out=prob_values[q_tile][:],
-                    in0=e_values[q_tile][:],
+                    out=prob_values[q_tile][:].rearrange("p (u c e) -> p u c e", u=2, e=2),
+                    in0=e_values[q_tile][:].rearrange("p (u e c) -> p u c e", u=2, e=2),
                     scalar1=inverse[:, a : a + 1],
                     scalar2=0.0,
                     op0=ALU.mult,
@@ -170,19 +170,18 @@ def tile_fake_sd_mha_model_pa_t_kernel(tc, mat1, mat2, mat3, bias, out):
         def transpose_prob(q_tile):
             pair, a = divmod(q_tile, 2)
             if a == 0:
-                prob_t_banks[pair] = psum.tile([P, 2, TILES, P], BF16, name="prob_t_bank", tag="prob_t_bank")
-            for t in range(TILES):
-                nc.tensor.transpose(
-                    prob_t_banks[pair][:, a, t, :], prob_values[q_tile][:, t * P : (t + 1) * P], ident_bf16[:]
-                )
+                prob_t_banks[pair] = psum.tile([P, 2, 2, P], F32, name="prob_t_bank", tag="prob_t_bank")
+            words = prob_values[q_tile][:].bitcast(F32)
+            for u in range(2):
+                nc.tensor.transpose(prob_t_banks[pair][:, a, u, :], words[:, u * P : (u + 1) * P], ident_f32[:])
 
         def copy_prob(pair):
-            grouped = work.tile([P, 2, P, TILES], BF16, name="prob_grouped", tag="prob_grouped", align_bytes=64)
-            nc.scalar.copy(out=grouped[:], in_=prob_t_banks[pair][:].rearrange("c a t p -> c a p t"))
+            grouped = work.tile([P, 2, P, 2], F32, name="prob_grouped", tag="prob_grouped", align_bytes=64)
+            nc.scalar.copy(out=grouped[:], in_=prob_t_banks[pair][:].rearrange("c a u p -> c a p u"))
             prob_grouped[pair] = grouped
 
         def quantise_prob(pair):
-            prob_mx[pair] = quantise(prob_grouped[pair][:].rearrange("c a p t -> c (a p t)"), 2 * P, "prob")
+            prob_mx[pair] = quantise(prob_grouped[pair][:].rearrange("c a p u -> c (a p u)").bitcast(BF16), 2 * P, "prob")
 
         def mx_passes(pair):
             prob_codes, prob_scales = prob_mx[pair]

@@ -249,12 +249,9 @@ def tile_fake_sd_mha_model_pa_t_kernel(tc, mat1, mat2, mat3, bias, out):
             scores_now = tile_behind(step, 0)
             pair_for_mx = pair_behind(step, MX_LAG)
             run(lambda q_tile: score_matmul(q_tile, 0), scores_now)
-            if pair_for_mx is None:
-                run(transpose_prob, tile_behind(step, PROB_TRANSPOSE_LAG))
             run(mx_passes, pair_for_mx)
             run(lambda q_tile: score_matmul(q_tile, 1), scores_now)
-            if pair_for_mx is not None:
-                run(transpose_prob, tile_behind(step, PROB_TRANSPOSE_LAG))
+            run(transpose_prob, tile_behind(step, PROB_TRANSPOSE_LAG))
             run(lambda head: transpose_words(q_rows, head), head_starting(step + Q_TRANSPOSE_LEAD))
             run(lambda head: transpose_words(k_rows, head), head_starting(step + K_TRANSPOSE_LEAD))
             run(add_bias, scores_now)

@@ -201,8 +201,7 @@ def tile_fake_sd_mha_model_pa_t_kernel(tc, mat1, mat2, mat3, bias, out):
         def store(pair):
             head, pair_of_head = divmod(pair, 2)
             result = work.tile([P, 2 * D], F32, name="result", tag="result")
-            copy = (nc.vector.tensor_copy, nc.scalar.copy)[pair_of_head]
-            copy(out=result[:], in_=out_banks[pair][:].rearrange("p a d -> p (a d)"))
+            nc.scalar.copy(out=result[:], in_=out_banks[pair][:].rearrange("p a d -> p (a d)"))
             nc.sync.dma_start(
                 out=rows_of(out, head)[:, pair_of_head * 2 * D : (pair_of_head + 1) * 2 * D], in_=result[:]
             )

@@ -62,7 +62,7 @@ def tile_fake_sd_mha_model_pa_t_kernel(tc, mat1, mat2, mat3, bias, out):
 
         def transpose_words(rows_by_head, head):
             words = rows_by_head[head][:].bitcast(F32)
-            bank = psum.tile([P, S], F32, name="qk_bank", tag="qk_bank", bufs=1)
+            bank = psum.tile([P, S], F32, name="qk_bank", tag="shared_bank", bufs=3)
             for j in range(TILES):
                 nc.tensor.transpose(bank[:, j * P : (j + 1) * P], words[:, j * P : (j + 1) * P], ident_f32[:])
             qk_banks[head] = bank
@@ -186,7 +186,7 @@ def tile_fake_sd_mha_model_pa_t_kernel(tc, mat1, mat2, mat3, bias, out):
         def mx_passes(pair):
             prob_codes, prob_scales = prob_mx[pair]
             v_codes, v_scales = v_mx[pair // 2]
-            out_banks[pair] = psum.tile([P, 2, D], F32, name="out_bank", tag="out_bank")
+            out_banks[pair] = psum.tile([P, 2, D], F32, name="out_bank", tag="shared_bank", bufs=3)
             for a in range(2):
                 nc.tensor.matmul_mx(
                     out=out_banks[pair][:, a, :],

@@ -44,6 +44,7 @@ def tile_fake_sd_mha_model_pa_t_kernel(tc, mat1, mat2, mat3, bias, out):
         bias_t = const.tile([P, TILES, TILES, P], F32, name="bias_t")
         table_warm_up = const.tile([P, 1], F32, name="table_warm_up")
 
+        bias_banks = {}
         q_rows, k_rows, v_rows, qk_banks, q_t, k_t, v_grouped, v_mx = {}, {}, {}, {}, {}, {}, {}, {}
         score_banks, neg_max, e_values, prob_values = {}, {}, {}, {}
         row_sums, prob_t_banks, prob_grouped, prob_mx, out_banks = {}, {}, {}, {}, {}
@@ -54,6 +55,12 @@ def tile_fake_sd_mha_model_pa_t_kernel(tc, mat1, mat2, mat3, bias, out):
         def load(tensor, rows_by_head, tag, head):
             rows_by_head[head] = raw.tile([P, TILES * D], BF16, name=tag, tag=tag)
             nc.sync.dma_start(out=rows_by_head[head][:], in_=rows_of(tensor, head))
+
+        def load_bias(half):
+            nc.sync.dma_start(
+                out=bias_rows[:, 2 * half : 2 * half + 2, :].rearrange("p j k -> p (j k)"),
+                in_=bias[0, 0].rearrange("(p j) k -> p (j k)", j=TILES)[:, 2 * half * S : (2 * half + 2) * S],
+            )
 
         def load_head(head):
             load(mat1, q_rows, "q_rows", head)
@@ -82,14 +89,15 @@ def tile_fake_sd_mha_model_pa_t_kernel(tc, mat1, mat2, mat3, bias, out):
             )
             k_t[head] = by_parity(words)
 
-        def transpose_bias():
-            for pair, copy in enumerate((nc.vector.tensor_copy, nc.scalar.copy)):
-                bank = psum.tile([P, 2, TILES, P], BF16, name="bias_bank", tag="prob_t_bank")
-                for a in range(2):
-                    keys_by_t = bias_rows[:, 2 * pair + a, :].rearrange("p (c t) -> p t c", t=TILES)
-                    for t in range(TILES):
-                        nc.tensor.transpose(bank[:, a, t, :], keys_by_t[:, t, :], ident_bf16[:])
-                copy(out=bias_t[:, 2 * pair : 2 * pair + 2], in_=bank[:])
+        def transpose_bias(j):
+            bias_banks[j] = psum.tile([P, TILES, P], BF16, name="bias_bank", tag="prob_t_bank")
+            keys_by_t = bias_rows[:, j, :].rearrange("p (c t) -> p t c", t=TILES)
+            for t in range(TILES):
+                nc.tensor.transpose(bias_banks[j][:, t, :], keys_by_t[:, t, :], ident_bf16[:])
+
+        def copy_bias(j):
+            copy = (nc.scalar.copy, nc.vector.tensor_copy)[j % 2]
+            copy(out=bias_t[:, j], in_=bias_banks[j][:])
 
         def regroup_v(head):
             grouped = work.tile([P, D, TILES], BF16, name="v_grouped", tag="v_grouped", align_bytes=64)
@@ -158,7 +166,8 @@ def tile_fake_sd_mha_model_pa_t_kernel(tc, mat1, mat2, mat3, bias, out):
             for a in range(2):
                 q_tile = 2 * pair + a
                 prob_values[q_tile] = long_work.tile([P, S], BF16, name="prob_values", tag="prob_values")
-                nc.gpsimd.tensor_scalar(
+                engine = nc.vector if q_tile == STEPS - 1 else nc.gpsimd
+                engine.tensor_scalar(
                     out=prob_values[q_tile][:].rearrange("p (u c e) -> p u c e", u=2, e=2),
                     in0=e_values[q_tile][:].rearrange("p (u e c) -> p u c e", u=2, e=2),
                     scalar1=inverse[:, a : a + 1],
@@ -200,8 +209,10 @@ def tile_fake_sd_mha_model_pa_t_kernel(tc, mat1, mat2, mat3, bias, out):
 
         def store(pair):
             head, pair_of_head = divmod(pair, 2)
-            result = work.tile([P, 2 * D], F32, name="result", tag="result")
-            nc.scalar.copy(out=result[:], in_=out_banks[pair][:].rearrange("p a d -> p (a d)"))
+            result = long_work.tile([P, 2 * D], F32, name="result", tag="result")
+            draining = 2 * pair + 1 + OUT_LAG > STEPS + MAX_LAG
+            copy = nc.vector.tensor_copy if draining and pair % 2 == 0 else nc.scalar.copy
+            copy(out=result[:], in_=out_banks[pair][:].rearrange("p a d -> p (a d)"))
             nc.sync.dma_start(
                 out=rows_of(out, head)[:, pair_of_head * 2 * D : (pair_of_head + 1) * 2 * D], in_=result[:]
             )
@@ -223,10 +234,9 @@ def tile_fake_sd_mha_model_pa_t_kernel(tc, mat1, mat2, mat3, bias, out):
 
         load(mat1, q_rows, "q_rows", 0)
         load(mat2, k_rows, "k_rows", 0)
-        nc.sync.dma_start(
-            out=bias_rows[:].rearrange("p j k -> p (j k)"), in_=bias[0, 0].rearrange("(p j) k -> p (j k)", j=TILES)
-        )
+        load_bias(0)
         load(mat1, q_rows, "q_rows", 1)
+        load_bias(1)
         load(mat2, k_rows, "k_rows", 1)
         load(mat3, v_rows, "v_rows", 0)
         load(mat3, v_rows, "v_rows", 1)
@@ -240,7 +250,9 @@ def tile_fake_sd_mha_model_pa_t_kernel(tc, mat1, mat2, mat3, bias, out):
         copy_q(0)
         transpose_words(k_rows, 0)
         copy_k(0)
-        transpose_bias()
+        for j in (0, 1):
+            transpose_bias(j)
+            copy_bias(j)
 
         for step in range(-1, STEPS + OUT_LAG + 1):
             run(load_head, head_starting(step + LOAD_LEAD))
@@ -254,13 +266,20 @@ def tile_fake_sd_mha_model_pa_t_kernel(tc, mat1, mat2, mat3, bias, out):
             run(lambda head: transpose_words(q_rows, head), head_starting(step + Q_TRANSPOSE_LEAD))
             run(lambda head: transpose_words(k_rows, head), head_starting(step + K_TRANSPOSE_LEAD))
             run(add_bias, scores_now)
+            if step == 0:
+                transpose_bias(2)
+                transpose_bias(3)
 
             run(exponential, tile_behind(step, EXP_LAG))
+            if step == 0:
+                copy_bias(2)
             run(copy_prob, pair_behind(step, PROB_COPY_LAG))
             run(copy_q, head_starting(step + Q_COPY_LEAD))
 
             run(normalise, pair_behind(step, NORM_LAG))
             run(row_max, tile_behind(step, MAX_LAG))
+            if step == 1:
+                copy_bias(3)
             run(copy_k, head_starting(step + K_COPY_LEAD))
             run(store, pair_behind(step, OUT_LAG))
             run(quantise_prob, pair_behind(step, PROB_QUANT_LAG))

@@ -24,6 +24,7 @@ Q_TRANSPOSE_LEAD, Q_COPY_LEAD, K_TRANSPOSE_LEAD, K_COPY_LEAD = 5, 4, 3, 2
 V_REGROUP_LAG, V_QUANT_LAG = 3, 7
 MAX_LAG, EXP_LAG, PROB_TRANSPOSE_LAG = 1, 2, 6
 NORM_LAG, PROB_COPY_LAG, PROB_QUANT_LAG, MX_LAG, OUT_LAG = 3, 7, 8, 11, 12
+WARM_UP_FIRST, WARM_UP_BETWEEN = 6, 1
 
 
 def tile_fake_sd_mha_model_pa_t_kernel(tc, mat1, mat2, mat3, bias, out):
@@ -43,6 +44,7 @@ def tile_fake_sd_mha_model_pa_t_kernel(tc, mat1, mat2, mat3, bias, out):
         bias_rows = const.tile([P, TILES, S], BF16, name="bias_rows")
         bias_t = const.tile([P, TILES, TILES, P], F32, name="bias_t")
         table_warm_up = const.tile([P, 1], F32, name="table_warm_up")
+        zeros = const.tile([P, S], BF16, name="zeros")
 
         bias_banks = {}
         q_rows, k_rows, v_rows, qk_banks, q_t, k_t, v_grouped, v_mx = {}, {}, {}, {}, {}, {}, {}, {}
@@ -217,6 +219,10 @@ def tile_fake_sd_mha_model_pa_t_kernel(tc, mat1, mat2, mat3, bias, out):
                 out=rows_of(out, head)[:, pair_of_head * 2 * D : (pair_of_head + 1) * 2 * D], in_=result[:]
             )
 
+        def warm_up(bank, count):
+            for repeat in range(count):
+                nc.tensor.matmul(bank[:], lhsT=zeros[:, :P], rhs=zeros[:], start=True, stop=True)
+
         def tile_behind(step, lag):
             return step - lag if 0 <= step - lag < STEPS else None
 
@@ -242,15 +248,19 @@ def tile_fake_sd_mha_model_pa_t_kernel(tc, mat1, mat2, mat3, bias, out):
         load(mat3, v_rows, "v_rows", 1)
         for head in range(2, LOAD_LEAD // TILES):
             load_head(head)
+        nc.vector.memset(zeros[:], 0.0)
         make_identity(nc, ident_f32[:])
         make_identity(nc, ident_bf16[:])
         nc.vector.memset(table_warm_up[:], 0.0)
         nc.scalar.activation(out=table_warm_up[:], in_=table_warm_up[:], func=ACT.Exp)
+        warm_bank = psum.tile([P, S], F32, name="warm_bank", tag="score_bank", bufs=3)
+        warm_up(warm_bank, WARM_UP_FIRST)
         transpose_words(q_rows, 0)
         copy_q(0)
         transpose_words(k_rows, 0)
         copy_k(0)
         for j in (0, 1):
+            warm_up(warm_bank, WARM_UP_BETWEEN)
             transpose_bias(j)
             copy_bias(j)
 

@@ -25,6 +25,9 @@ V_REGROUP_LAG, V_QUANT_LAG = 3, 7
 MAX_LAG, EXP_LAG, PROB_TRANSPOSE_LAG = 1, 2, 6
 NORM_LAG, PROB_COPY_LAG, PROB_QUANT_LAG, MX_LAG, OUT_LAG = 3, 7, 8, 11, 12
 WARM_UP_FIRST, WARM_UP_BETWEEN = 6, 1
+PIECES = 3
+PIECE_EDGES = [2 * ((S * piece) // (2 * PIECES)) for piece in range(PIECES + 1)]
+BIAS_FIRST_FROM = 1
 
 
 def tile_fake_sd_mha_model_pa_t_kernel(tc, mat1, mat2, mat3, bias, out):
@@ -37,7 +40,7 @@ def tile_fake_sd_mha_model_pa_t_kernel(tc, mat1, mat2, mat3, bias, out):
         work = ctx.enter_context(tc.tile_pool(name="work", bufs=4))
         long_work = ctx.enter_context(tc.tile_pool(name="long_work", bufs=6))
         small = ctx.enter_context(tc.tile_pool(name="small", bufs=8))
-        psum = ctx.enter_context(tc.psum_pool(name="psum", bufs=2))
+        psum = ctx.enter_context(tc.psum_pool(name="psum", bufs=4))
 
         ident_f32 = const.tile([P, P], F32, name="ident_f32")
         ident_bf16 = const.tile([P, P], BF16, name="ident_bf16")
@@ -69,12 +72,11 @@ def tile_fake_sd_mha_model_pa_t_kernel(tc, mat1, mat2, mat3, bias, out):
             load(mat2, k_rows, "k_rows", head)
             load(mat3, v_rows, "v_rows", head)
 
-        def transpose_words(rows_by_head, head):
+        def transpose_words(rows_by_head, head, j):
+            if j == 0:
+                qk_banks[head] = psum.tile([P, S], F32, name="qk_bank", tag="shared_bank")
             words = rows_by_head[head][:].bitcast(F32)
-            bank = psum.tile([P, S], F32, name="qk_bank", tag="shared_bank", bufs=3)
-            for j in range(TILES):
-                nc.tensor.transpose(bank[:, j * P : (j + 1) * P], words[:, j * P : (j + 1) * P], ident_f32[:])
-            qk_banks[head] = bank
+            nc.tensor.transpose(qk_banks[head][:, j * P : (j + 1) * P], words[:, j * P : (j + 1) * P], ident_f32[:])
 
         def by_parity(words):
             return words[:].bitcast(BF16).rearrange("w (row parity) -> w row parity", parity=2)
@@ -92,7 +94,7 @@ def tile_fake_sd_mha_model_pa_t_kernel(tc, mat1, mat2, mat3, bias, out):
             k_t[head] = by_parity(words)
 
         def transpose_bias(j):
-            bias_banks[j] = psum.tile([P, TILES, P], BF16, name="bias_bank", tag="prob_t_bank")
+            bias_banks[j] = psum.tile([P, TILES, P], BF16, name="bias_bank", tag="shared_bank")
             keys_by_t = bias_rows[:, j, :].rearrange("p (c t) -> p t c", t=TILES)
             for t in range(TILES):
                 nc.tensor.transpose(bias_banks[j][:, t, :], keys_by_t[:, t, :], ident_bf16[:])
@@ -118,29 +120,35 @@ def tile_fake_sd_mha_model_pa_t_kernel(tc, mat1, mat2, mat3, bias, out):
         def quantise_v(head):
             v_mx[head] = quantise(v_grouped[head][:].rearrange("p d t -> p (d t)"), D, "v")
 
-        def score_matmul(q_tile, parity):
+        def open_score_bank(q_tile):
+            score_banks[q_tile] = psum.tile([P, S], F32, name="score_bank", tag="score_bank")
+
+        def score_matmul(q_tile, parity, piece):
             head, j = divmod(q_tile, TILES)
-            if parity == 0:
-                score_banks[q_tile] = psum.tile([P, S], F32, name="score_bank", tag="score_bank", bufs=3)
+            bias_last = q_tile < BIAS_FIRST_FROM
+            if bias_last and parity == 0 and piece == 0:
+                open_score_bank(q_tile)
+            columns = slice(PIECE_EDGES[piece], PIECE_EDGES[piece + 1])
             nc.tensor.matmul(
-                score_banks[q_tile][:],
+                score_banks[q_tile][:, columns],
                 lhsT=q_t[head][:, j * P : (j + 1) * P, parity],
-                rhs=k_t[head][:, :, parity],
-                start=(parity == 0),
-                stop=False,
+                rhs=k_t[head][:, columns, parity],
+                start=(bias_last and parity == 0 and piece == 0),
+                stop=(not bias_last and parity == 1 and piece == PIECES - 1),
             )
 
-        def add_bias(q_tile):
-            j = q_tile % TILES
-            for t in range(TILES):
-                nc.tensor.matmul(
-                    score_banks[q_tile][:, t * P : (t + 1) * P],
-                    lhsT=bias_t[:, j, t, :],
-                    rhs=ident_f32[:],
-                    is_transpose=True,
-                    start=False,
-                    stop=(t == TILES - 1),
-                )
+        def bias_transpose(q_tile, t):
+            bias_last = q_tile < BIAS_FIRST_FROM
+            if not bias_last and t == 0:
+                open_score_bank(q_tile)
+            nc.tensor.matmul(
+                score_banks[q_tile][:, t * P : (t + 1) * P],
+                lhsT=bias_t[:, q_tile % TILES, t, :],
+                rhs=ident_f32[:],
+                is_transpose=True,
+                start=(not bias_last and t == 0),
+                stop=(bias_last and t == TILES - 1),
+            )
 
         def row_max(q_tile):
             neg_max[q_tile] = small.tile([P, 1], F32, name="neg_max", tag="neg_max")
@@ -178,13 +186,12 @@ def tile_fake_sd_mha_model_pa_t_kernel(tc, mat1, mat2, mat3, bias, out):
                     op1=ALU.add,
                 )
 
-        def transpose_prob(q_tile):
+        def transpose_prob(q_tile, u):
             pair, a = divmod(q_tile, 2)
-            if a == 0:
-                prob_t_banks[pair] = psum.tile([P, 2, 2, P], F32, name="prob_t_bank", tag="prob_t_bank")
+            if a == 0 and u == 0:
+                prob_t_banks[pair] = psum.tile([P, 2, 2, P], F32, name="prob_t_bank", tag="shared_bank")
             words = prob_values[q_tile][:].bitcast(F32)
-            for u in range(2):
-                nc.tensor.transpose(prob_t_banks[pair][:, a, u, :], words[:, u * P : (u + 1) * P], ident_f32[:])
+            nc.tensor.transpose(prob_t_banks[pair][:, a, u, :], words[:, u * P : (u + 1) * P], ident_f32[:])
 
         def copy_prob(pair):
             grouped = work.tile([P, 2, P, 2], F32, name="prob_grouped", tag="prob_grouped", align_bytes=64)
@@ -197,7 +204,7 @@ def tile_fake_sd_mha_model_pa_t_kernel(tc, mat1, mat2, mat3, bias, out):
         def mx_passes(pair):
             prob_codes, prob_scales = prob_mx[pair]
             v_codes, v_scales = v_mx[pair // 2]
-            out_banks[pair] = psum.tile([P, 2, D], F32, name="out_bank", tag="shared_bank", bufs=3)
+            out_banks[pair] = psum.tile([P, 2, D], F32, name="out_bank", tag="shared_bank")
             for a in range(2):
                 nc.tensor.matmul_mx(
                     out=out_banks[pair][:, a, :],
@@ -253,31 +260,55 @@ def tile_fake_sd_mha_model_pa_t_kernel(tc, mat1, mat2, mat3, bias, out):
         make_identity(nc, ident_bf16[:])
         nc.vector.memset(table_warm_up[:], 0.0)
         nc.scalar.activation(out=table_warm_up[:], in_=table_warm_up[:], func=ACT.Exp)
-        warm_bank = psum.tile([P, S], F32, name="warm_bank", tag="score_bank", bufs=3)
+        warm_bank = psum.tile([P, S], F32, name="warm_bank", tag="score_bank")
         warm_up(warm_bank, WARM_UP_FIRST)
-        transpose_words(q_rows, 0)
+        for j in range(TILES):
+            transpose_words(q_rows, 0, j)
         copy_q(0)
-        transpose_words(k_rows, 0)
+        for j in range(TILES):
+            transpose_words(k_rows, 0, j)
         copy_k(0)
         for j in (0, 1):
             warm_up(warm_bank, WARM_UP_BETWEEN)
             transpose_bias(j)
             copy_bias(j)
 
-        for step in range(-1, STEPS + OUT_LAG + 1):
+        for step in range(STEPS + OUT_LAG + 1):
             run(load_head, head_starting(step + LOAD_LEAD))
 
             scores_now = tile_behind(step, 0)
             pair_for_mx = pair_behind(step, MX_LAG)
-            run(lambda q_tile: score_matmul(q_tile, 0), scores_now)
-            run(mx_passes, pair_for_mx)
-            run(lambda q_tile: score_matmul(q_tile, 1), scores_now)
-            run(transpose_prob, tile_behind(step, PROB_TRANSPOSE_LAG))
-            run(lambda head: transpose_words(q_rows, head), head_starting(step + Q_TRANSPOSE_LEAD))
-            run(lambda head: transpose_words(k_rows, head), head_starting(step + K_TRANSPOSE_LEAD))
-            run(add_bias, scores_now)
+            matmuls = []
+            for parity in range(2):
+                if scores_now is not None:
+                    for piece in range(PIECES):
+                        before_mx = pair_for_mx is not None and parity == 0 and piece == PIECES - 1
+                        matmuls.append((score_matmul, (scores_now, parity, piece), not before_mx))
+                if parity == 0 and pair_for_mx is not None:
+                    matmuls.append((mx_passes, (pair_for_mx,), scores_now is None))
+            transposes = []
+            for rows_by_head, lead in ((q_rows, Q_TRANSPOSE_LEAD), (k_rows, K_TRANSPOSE_LEAD)):
+                head = head_starting(step + lead) if step > 0 else head_starting(step + lead - 1)
+                if head is not None:
+                    transposes.extend([(transpose_words, (rows_by_head, head, j)) for j in range(TILES)])
+            scores_next = tile_behind(step + 1, 0)
+            if scores_next is not None and scores_next >= BIAS_FIRST_FROM:
+                transposes.extend([(bias_transpose, (scores_next, t)) for t in range(TILES)])
+            prob_now = tile_behind(step, PROB_TRANSPOSE_LAG)
+            if prob_now is not None:
+                transposes.extend([(transpose_prob, (prob_now, u)) for u in range(2)])
+            woven = 0
+            for stage, arguments, transposition_may_follow in matmuls:
+                stage(*arguments)
+                if transposition_may_follow and woven < len(transposes):
+                    transposes[woven][0](*transposes[woven][1])
+                    woven += 1
+            for stage, arguments in transposes[woven:]:
+                stage(*arguments)
             if step == 0:
                 transpose_bias(2)
+                for t in range(TILES):
+                    bias_transpose(scores_now, t)
                 transpose_bias(3)
 
             run(exponential, tile_behind(step, EXP_LAG))

@@ -25,8 +25,6 @@ V_REGROUP_LAG, V_QUANT_LAG = 3, 7
 MAX_LAG, EXP_LAG, PROB_TRANSPOSE_LAG = 1, 2, 6
 NORM_LAG, PROB_COPY_LAG, PROB_QUANT_LAG, MX_LAG, OUT_LAG = 3, 7, 8, 11, 12
 WARM_UP_FIRST, WARM_UP_BETWEEN = 6, 1
-PIECES = 3
-PIECE_EDGES = [2 * ((S * piece) // (2 * PIECES)) for piece in range(PIECES + 1)]
 BIAS_FIRST_FROM = 1
 
 
@@ -123,18 +121,17 @@ def tile_fake_sd_mha_model_pa_t_kernel(tc, mat1, mat2, mat3, bias, out):
         def open_score_bank(q_tile):
             score_banks[q_tile] = psum.tile([P, S], F32, name="score_bank", tag="score_bank")
 
-        def score_matmul(q_tile, parity, piece):
+        def score_matmul(q_tile, parity):
             head, j = divmod(q_tile, TILES)
             bias_last = q_tile < BIAS_FIRST_FROM
-            if bias_last and parity == 0 and piece == 0:
+            if bias_last and parity == 0:
                 open_score_bank(q_tile)
-            columns = slice(PIECE_EDGES[piece], PIECE_EDGES[piece + 1])
             nc.tensor.matmul(
-                score_banks[q_tile][:, columns],
+                score_banks[q_tile][:],
                 lhsT=q_t[head][:, j * P : (j + 1) * P, parity],
-                rhs=k_t[head][:, columns, parity],
-                start=(bias_last and parity == 0 and piece == 0),
-                stop=(not bias_last and parity == 1 and piece == PIECES - 1),
+                rhs=k_t[head][:, :, parity],
+                start=(bias_last and parity == 0),
+                stop=(not bias_last and parity == 1),
             )
 
         def bias_transpose(q_tile, t):
@@ -277,34 +274,22 @@ def tile_fake_sd_mha_model_pa_t_kernel(tc, mat1, mat2, mat3, bias, out):
             run(load_head, head_starting(step + LOAD_LEAD))
 
             scores_now = tile_behind(step, 0)
-            pair_for_mx = pair_behind(step, MX_LAG)
-            matmuls = []
-            for parity in range(2):
-                if scores_now is not None:
-                    for piece in range(PIECES):
-                        before_mx = pair_for_mx is not None and parity == 0 and piece == PIECES - 1
-                        matmuls.append((score_matmul, (scores_now, parity, piece), not before_mx))
-                if parity == 0 and pair_for_mx is not None:
-                    matmuls.append((mx_passes, (pair_for_mx,), scores_now is None))
-            transposes = []
+            scores_next = tile_behind(step + 1, 0)
+            prob_now = tile_behind(step, PROB_TRANSPOSE_LAG)
+            run(lambda q_tile: score_matmul(q_tile, 0), scores_now)
+            run(mx_passes, pair_behind(step, MX_LAG))
+            run(lambda q_tile: score_matmul(q_tile, 1), scores_now)
             for rows_by_head, lead in ((q_rows, Q_TRANSPOSE_LEAD), (k_rows, K_TRANSPOSE_LEAD)):
                 head = head_starting(step + lead) if step > 0 else head_starting(step + lead - 1)
                 if head is not None:
-                    transposes.extend([(transpose_words, (rows_by_head, head, j)) for j in range(TILES)])
-            scores_next = tile_behind(step + 1, 0)
+                    for j in range(TILES):
+                        transpose_words(rows_by_head, head, j)
             if scores_next is not None and scores_next >= BIAS_FIRST_FROM:
-                transposes.extend([(bias_transpose, (scores_next, t)) for t in range(TILES)])
-            prob_now = tile_behind(step, PROB_TRANSPOSE_LAG)
+                for t in range(TILES):
+                    bias_transpose(scores_next, t)
             if prob_now is not None:
-                transposes.extend([(transpose_prob, (prob_now, u)) for u in range(2)])
-            woven = 0
-            for stage, arguments, transposition_may_follow in matmuls:
-                stage(*arguments)
-                if transposition_may_follow and woven < len(transposes):
-                    transposes[woven][0](*transposes[woven][1])
-                    woven += 1
-            for stage, arguments in transposes[woven:]:
-                stage(*arguments)
+                for u in range(2):
+                    transpose_prob(prob_now, u)
             if step == 0:
                 transpose_bias(2)
                 for t in range(TILES):

@@ -22,6 +22,7 @@ FLOPS = 2 * 2 * HEADS * S * S * D
 LOAD_LEAD = 4 * TILES
 Q_TRANSPOSE_LEAD, Q_COPY_LEAD, K_TRANSPOSE_LEAD, K_COPY_LEAD = 5, 4, 3, 2
 V_REGROUP_LAG, V_QUANT_LAG = 3, 7
+V_EARLY_HEADS, V_EARLY_STEPS = 3, 6
 MAX_LAG, EXP_LAG, PROB_TRANSPOSE_LAG = 1, 2, 6
 NORM_LAG, PROB_COPY_LAG, PROB_QUANT_LAG, MX_LAG, OUT_LAG = 3, 7, 8, 11, 12
 WARM_UP_FIRST, WARM_UP_BETWEEN = 6, 1
@@ -173,7 +174,7 @@ def tile_fake_sd_mha_model_pa_t_kernel(tc, mat1, mat2, mat3, bias, out):
             for a in range(2):
                 q_tile = 2 * pair + a
                 prob_values[q_tile] = long_work.tile([P, S], BF16, name="prob_values", tag="prob_values")
-                engine = nc.vector if q_tile == STEPS - 1 else nc.gpsimd
+                engine = nc.vector if pair == STEPS // 2 - 1 else nc.gpsimd
                 engine.tensor_scalar(
                     out=prob_values[q_tile][:].rearrange("p (u c e) -> p u c e", u=2, e=2),
                     in0=e_values[q_tile][:].rearrange("p (u e c) -> p u c e", u=2, e=2),
@@ -216,7 +217,7 @@ def tile_fake_sd_mha_model_pa_t_kernel(tc, mat1, mat2, mat3, bias, out):
         def store(pair):
             head, pair_of_head = divmod(pair, 2)
             result = long_work.tile([P, 2 * D], F32, name="result", tag="result")
-            draining = 2 * pair + 1 + OUT_LAG > STEPS + MAX_LAG
+            draining = 2 * pair + 1 + OUT_LAG >= STEPS + MAX_LAG
             copy = nc.vector.tensor_copy if draining and pair % 2 == 0 else nc.scalar.copy
             copy(out=result[:], in_=out_banks[pair][:].rearrange("p a d -> p (a d)"))
             nc.sync.dma_start(
@@ -237,6 +238,13 @@ def tile_fake_sd_mha_model_pa_t_kernel(tc, mat1, mat2, mat3, bias, out):
         def head_starting(step):
             head, j = divmod(step, TILES)
             return head if j == 0 and 0 <= head < HEADS else None
+
+        def head_for_v(step, lag):
+            for head in range(HEADS):
+                early = V_EARLY_STEPS if head >= HEADS - V_EARLY_HEADS else 0
+                if step == TILES * head + lag - early:
+                    return head
+            return None
 
         def run(stage, index):
             if index is not None:
@@ -309,5 +317,5 @@ def tile_fake_sd_mha_model_pa_t_kernel(tc, mat1, mat2, mat3, bias, out):
             run(copy_k, head_starting(step + K_COPY_LEAD))
             run(store, pair_behind(step, OUT_LAG))
             run(quantise_prob, pair_behind(step, PROB_QUANT_LAG))
-            run(quantise_v, head_starting(step - V_QUANT_LAG))
-            run(regroup_v, head_starting(step - V_REGROUP_LAG))
+            run(quantise_v, head_for_v(step, V_QUANT_LAG))
+            run(regroup_v, head_for_v(step, V_REGROUP_LAG))

@@ -160,8 +160,8 @@ def tile_fake_sd_mha_model_pa_t_kernel(tc, mat1, mat2, mat3, bias, out):
                 row_sums[pair] = small.tile([P, 2], F32, name="row_sums", tag="row_sums")
             e_values[q_tile] = long_work.tile([P, S], F32, name="e_values", tag="e_values")
             nc.scalar.activation(
-                out=e_values[q_tile][:],
-                in_=score_banks[q_tile][:],
+                out=e_values[q_tile][:].rearrange("p (u c e) -> p u c e", u=2, e=2),
+                in_=score_banks[q_tile][:].rearrange("p (u e c) -> p u c e", u=2, e=2),
                 func=ACT.Exp,
                 bias=neg_max[q_tile][:],
                 scale=1.0,
@@ -176,8 +176,8 @@ def tile_fake_sd_mha_model_pa_t_kernel(tc, mat1, mat2, mat3, bias, out):
                 prob_values[q_tile] = long_work.tile([P, S], BF16, name="prob_values", tag="prob_values")
                 engine = nc.vector if pair == STEPS // 2 - 1 else nc.gpsimd
                 engine.tensor_scalar(
-                    out=prob_values[q_tile][:].rearrange("p (u c e) -> p u c e", u=2, e=2),
-                    in0=e_values[q_tile][:].rearrange("p (u e c) -> p u c e", u=2, e=2),
+                    out=prob_values[q_tile][:],
+                    in0=e_values[q_tile][:],
                     scalar1=inverse[:, a : a + 1],
                     scalar2=0.0,
                     op0=ALU.mult,

@@ -21,7 +21,7 @@ FLOPS = 2 * 2 * HEADS * S * S * D
 
 LOAD_LEAD = 4 * TILES
 Q_TRANSPOSE_LEAD, Q_COPY_LEAD, K_TRANSPOSE_LEAD, K_COPY_LEAD = 5, 4, 3, 2
-V_REGROUP_LAG, V_QUANT_LAG = 3, 7
+V_REGROUP_LAG, V_QUANT_LAG = 3, 5
 V_EARLY_HEADS, V_EARLY_STEPS = 3, 6
 MAX_LAG, EXP_LAG, PROB_TRANSPOSE_LAG = 1, 2, 6
 NORM_LAG, PROB_COPY_LAG, PROB_QUANT_LAG, MX_LAG, OUT_LAG = 3, 7, 8, 11, 12

@@ -25,7 +25,7 @@ V_REGROUP_LAG, V_QUANT_LAG = 3, 5
 V_EARLY_HEADS, V_EARLY_STEPS = 3, 6
 MAX_LAG, EXP_LAG, PROB_TRANSPOSE_LAG = 1, 2, 6
 NORM_LAG, PROB_COPY_LAG, PROB_QUANT_LAG, MX_LAG, OUT_LAG = 3, 7, 8, 11, 12
-WARM_UP_FIRST, WARM_UP_BETWEEN = 6, 1
+WARM_UP_FIRST, WARM_UP_BETWEEN = 4, 1
 BIAS_FIRST_FROM = 1
 
 

from contextlib import ExitStack

import concourse.mybir as mybir
from concourse.masks import make_identity

F32 = mybir.dt.float32
BF16 = mybir.dt.bfloat16
U32 = mybir.dt.uint32
U8 = mybir.dt.uint8
FP8X4 = mybir.dt.float8_e4m3fn_x4
ALU = mybir.AluOpType
ACT = mybir.ActivationFunctionType
AX = mybir.AxisListType

P = 128
HEADS_PER_BATCH, S, D = 2, 512, 256
HEADS = 16
TILES = S // P
STEPS = HEADS * TILES
FLOPS = 2 * 2 * HEADS * S * S * D

LOAD_LEAD = 4 * TILES
Q_TRANSPOSE_LEAD, Q_COPY_LEAD, K_TRANSPOSE_LEAD, K_COPY_LEAD = 5, 4, 3, 2
V_REGROUP_LAG, V_QUANT_LAG = 3, 5
V_EARLY_HEADS, V_EARLY_STEPS = 3, 6
MAX_LAG, EXP_LAG, PROB_TRANSPOSE_LAG = 1, 2, 6
NORM_LAG, PROB_COPY_LAG, PROB_QUANT_LAG, MX_LAG, OUT_LAG = 3, 7, 8, 11, 12
WARM_UP_FIRST, WARM_UP_BETWEEN = 4, 1
BIAS_FIRST_FROM = 1


def tile_fake_sd_mha_model_pa_t_kernel(tc, mat1, mat2, mat3, bias, out):
    nc = tc.nc

    with ExitStack() as ctx:
        ctx.enter_context(tc.manual_schedule())
        const = ctx.enter_context(tc.tile_pool(name="const", bufs=1))
        raw = ctx.enter_context(tc.tile_pool(name="raw", bufs=6))
        work = ctx.enter_context(tc.tile_pool(name="work", bufs=4))
        long_work = ctx.enter_context(tc.tile_pool(name="long_work", bufs=6))
        small = ctx.enter_context(tc.tile_pool(name="small", bufs=8))
        psum = ctx.enter_context(tc.psum_pool(name="psum", bufs=4))

        ident_f32 = const.tile([P, P], F32, name="ident_f32")
        ident_bf16 = const.tile([P, P], BF16, name="ident_bf16")
        bias_rows = const.tile([P, TILES, S], BF16, name="bias_rows")
        bias_t = const.tile([P, TILES, TILES, P], F32, name="bias_t")
        table_warm_up = const.tile([P, 1], F32, name="table_warm_up")
        zeros = const.tile([P, S], BF16, name="zeros")

        bias_banks = {}
        q_rows, k_rows, v_rows, qk_banks, q_t, k_t, v_grouped, v_mx = {}, {}, {}, {}, {}, {}, {}, {}
        score_banks, neg_max, e_values, prob_values = {}, {}, {}, {}
        row_sums, prob_t_banks, prob_grouped, prob_mx, out_banks = {}, {}, {}, {}, {}

        def rows_of(tensor, head):
            return tensor[head // HEADS_PER_BATCH, head % HEADS_PER_BATCH].rearrange("(p j) d -> p (j d)", j=TILES)

        def load(tensor, rows_by_head, tag, head):
            rows_by_head[head] = raw.tile([P, TILES * D], BF16, name=tag, tag=tag)
            nc.sync.dma_start(out=rows_by_head[head][:], in_=rows_of(tensor, head))

        def load_bias(half):
            nc.sync.dma_start(
                out=bias_rows[:, 2 * half : 2 * half + 2, :].rearrange("p j k -> p (j k)"),
                in_=bias[0, 0].rearrange("(p j) k -> p (j k)", j=TILES)[:, 2 * half * S : (2 * half + 2) * S],
            )

        def load_head(head):
            load(mat1, q_rows, "q_rows", head)
            load(mat2, k_rows, "k_rows", head)
            load(mat3, v_rows, "v_rows", head)

        def transpose_words(rows_by_head, head, j):
            if j == 0:
                qk_banks[head] = psum.tile([P, S], F32, name="qk_bank", tag="shared_bank")
            words = rows_by_head[head][:].bitcast(F32)
            nc.tensor.transpose(qk_banks[head][:, j * P : (j + 1) * P], words[:, j * P : (j + 1) * P], ident_f32[:])

        def by_parity(words):
            return words[:].bitcast(BF16).rearrange("w (row parity) -> w row parity", parity=2)

        def copy_q(head):
            words = work.tile([P, S], F32, name="q_t", tag="q_t")
            nc.scalar.copy(out=words[:], in_=qk_banks[head][:])
            q_t[head] = by_parity(words)

        def copy_k(head):
            words = work.tile([P, S], F32, name="k_t", tag="k_t")
            nc.vector.tensor_scalar_mul(
                out=words[:].bitcast(BF16), in0=qk_banks[head][:].bitcast(BF16), scalar1=1.0 / 16.0
            )
            k_t[head] = by_parity(words)

        def transpose_bias(j):
            bias_banks[j] = psum.tile([P, TILES, P], BF16, name="bias_bank", tag="shared_bank")
            keys_by_t = bias_rows[:, j, :].rearrange("p (c t) -> p t c", t=TILES)
            for t in range(TILES):
                nc.tensor.transpose(bias_banks[j][:, t, :], keys_by_t[:, t, :], ident_bf16[:])

        def copy_bias(j):
            copy = (nc.scalar.copy, nc.vector.tensor_copy)[j % 2]
            copy(out=bias_t[:, j], in_=bias_banks[j][:])

        def regroup_v(head):
            grouped = work.tile([P, D, TILES], BF16, name="v_grouped", tag="v_grouped", align_bytes=64)
            nc.vector.tensor_copy(
                out=grouped[:].rearrange("p (run i) t -> p run t i", i=4),
                in_=v_rows[head][:].rearrange("p (t run i) -> p run t i", t=TILES, i=4),
            )
            v_grouped[head] = grouped

        def quantise(grouped, columns, tag):
            codes = work.tile([P, columns], U32, name=tag + "_codes", tag=tag + "_codes", align_bytes=64)
            scales = work.tile([P, columns], U8, name=tag + "_scales", tag=tag + "_scales", align_bytes=64)
            nc.vector.quantize_mx(out=codes[:].bitcast(FP8X4), scales=scales[:], in_=grouped)
            return codes, scales

        def quantise_v(head):
            v_mx[head] = quantise(v_grouped[head][:].rearrange("p d t -> p (d t)"), D, "v")

        def open_score_bank(q_tile):
            score_banks[q_tile] = psum.tile([P, S], F32, name="score_bank", tag="score_bank")

        def score_matmul(q_tile, parity):
            head, j = divmod(q_tile, TILES)
            bias_last = q_tile < BIAS_FIRST_FROM
            if bias_last and parity == 0:
                open_score_bank(q_tile)
            nc.tensor.matmul(
                score_banks[q_tile][:],
                lhsT=q_t[head][:, j * P : (j + 1) * P, parity],
                rhs=k_t[head][:, :, parity],
                start=(bias_last and parity == 0),
                stop=(not bias_last and parity == 1),
            )

        def bias_transpose(q_tile, t):
            bias_last = q_tile < BIAS_FIRST_FROM
            if not bias_last and t == 0:
                open_score_bank(q_tile)
            nc.tensor.matmul(
                score_banks[q_tile][:, t * P : (t + 1) * P],
                lhsT=bias_t[:, q_tile % TILES, t, :],
                rhs=ident_f32[:],
                is_transpose=True,
                start=(not bias_last and t == 0),
                stop=(bias_last and t == TILES - 1),
            )

        def row_max(q_tile):
            neg_max[q_tile] = small.tile([P, 1], F32, name="neg_max", tag="neg_max")
            nc.vector.tensor_reduce(
                out=neg_max[q_tile][:], in_=score_banks[q_tile][:], axis=AX.X, op=ALU.max, negate=True
            )

        def exponential(q_tile):
            pair, a = divmod(q_tile, 2)
            if a == 0:
                row_sums[pair] = small.tile([P, 2], F32, name="row_sums", tag="row_sums")
            e_values[q_tile] = long_work.tile([P, S], F32, name="e_values", tag="e_values")
            nc.scalar.activation(
                out=e_values[q_tile][:].rearrange("p (u c e) -> p u c e", u=2, e=2),
                in_=score_banks[q_tile][:].rearrange("p (u e c) -> p u c e", u=2, e=2),
                func=ACT.Exp,
                bias=neg_max[q_tile][:],
                scale=1.0,
                accum_out=row_sums[pair][:, a : a + 1],
            )

        def normalise(pair):
            inverse = small.tile([P, 2], F32, name="inverse", tag="inverse")
            nc.vector.reciprocal(inverse[:], row_sums[pair][:])
            for a in range(2):
                q_tile = 2 * pair + a
                prob_values[q_tile] = long_work.tile([P, S], BF16, name="prob_values", tag="prob_values")
                engine = nc.vector if pair == STEPS // 2 - 1 else nc.gpsimd
                engine.tensor_scalar(
                    out=prob_values[q_tile][:],
                    in0=e_values[q_tile][:],
                    scalar1=inverse[:, a : a + 1],
                    scalar2=0.0,
                    op0=ALU.mult,
                    op1=ALU.add,
                )

        def transpose_prob(q_tile, u):
            pair, a = divmod(q_tile, 2)
            if a == 0 and u == 0:
                prob_t_banks[pair] = psum.tile([P, 2, 2, P], F32, name="prob_t_bank", tag="shared_bank")
            words = prob_values[q_tile][:].bitcast(F32)
            nc.tensor.transpose(prob_t_banks[pair][:, a, u, :], words[:, u * P : (u + 1) * P], ident_f32[:])

        def copy_prob(pair):
            grouped = work.tile([P, 2, P, 2], F32, name="prob_grouped", tag="prob_grouped", align_bytes=64)
            nc.scalar.copy(out=grouped[:], in_=prob_t_banks[pair][:].rearrange("c a u p -> c a p u"))
            prob_grouped[pair] = grouped

        def quantise_prob(pair):
            prob_mx[pair] = quantise(prob_grouped[pair][:].rearrange("c a p u -> c (a p u)").bitcast(BF16), 2 * P, "prob")

        def mx_passes(pair):
            prob_codes, prob_scales = prob_mx[pair]
            v_codes, v_scales = v_mx[pair // 2]
            out_banks[pair] = psum.tile([P, 2, D], F32, name="out_bank", tag="shared_bank")
            for a in range(2):
                nc.tensor.matmul_mx(
                    out=out_banks[pair][:, a, :],
                    lhsT=prob_codes[:, a * P : (a + 1) * P].bitcast(FP8X4),
                    lhsT_scale=prob_scales[:, a * P : (a + 1) * P],
                    rhs=v_codes[:].bitcast(FP8X4),
                    rhs_scale=v_scales[:],
                    start=True,
                    stop=True,
                )

        def store(pair):
            head, pair_of_head = divmod(pair, 2)
            result = long_work.tile([P, 2 * D], F32, name="result", tag="result")
            draining = 2 * pair + 1 + OUT_LAG >= STEPS + MAX_LAG
            copy = nc.vector.tensor_copy if draining and pair % 2 == 0 else nc.scalar.copy
            copy(out=result[:], in_=out_banks[pair][:].rearrange("p a d -> p (a d)"))
            nc.sync.dma_start(
                out=rows_of(out, head)[:, pair_of_head * 2 * D : (pair_of_head + 1) * 2 * D], in_=result[:]
            )

        def warm_up(bank, count):
            for repeat in range(count):
                nc.tensor.matmul(bank[:], lhsT=zeros[:, :P], rhs=zeros[:], start=True, stop=True)

        def tile_behind(step, lag):
            return step - lag if 0 <= step - lag < STEPS else None

        def pair_behind(step, lag):
            q_tile = tile_behind(step, lag)
            return q_tile // 2 if q_tile is not None and q_tile % 2 == 1 else None

        def head_starting(step):
            head, j = divmod(step, TILES)
            return head if j == 0 and 0 <= head < HEADS else None

        def head_for_v(step, lag):
            for head in range(HEADS):
                early = V_EARLY_STEPS if head >= HEADS - V_EARLY_HEADS else 0
                if step == TILES * head + lag - early:
                    return head
            return None

        def run(stage, index):
            if index is not None:
                stage(index)

        load(mat1, q_rows, "q_rows", 0)
        load(mat2, k_rows, "k_rows", 0)
        load_bias(0)
        load(mat1, q_rows, "q_rows", 1)
        load_bias(1)
        load(mat2, k_rows, "k_rows", 1)
        load(mat3, v_rows, "v_rows", 0)
        load(mat3, v_rows, "v_rows", 1)
        for head in range(2, LOAD_LEAD // TILES):
            load_head(head)
        nc.vector.memset(zeros[:], 0.0)
        make_identity(nc, ident_f32[:])
        make_identity(nc, ident_bf16[:])
        nc.vector.memset(table_warm_up[:], 0.0)
        nc.scalar.activation(out=table_warm_up[:], in_=table_warm_up[:], func=ACT.Exp)
        warm_bank = psum.tile([P, S], F32, name="warm_bank", tag="score_bank")
        warm_up(warm_bank, WARM_UP_FIRST)
        for j in range(TILES):
            transpose_words(q_rows, 0, j)
        copy_q(0)
        for j in range(TILES):
            transpose_words(k_rows, 0, j)
        copy_k(0)
        for j in (0, 1):
            warm_up(warm_bank, WARM_UP_BETWEEN)
            transpose_bias(j)
            copy_bias(j)

        for step in range(STEPS + OUT_LAG + 1):
            run(load_head, head_starting(step + LOAD_LEAD))

            scores_now = tile_behind(step, 0)
            scores_next = tile_behind(step + 1, 0)
            prob_now = tile_behind(step, PROB_TRANSPOSE_LAG)
            run(lambda q_tile: score_matmul(q_tile, 0), scores_now)
            run(mx_passes, pair_behind(step, MX_LAG))
            run(lambda q_tile: score_matmul(q_tile, 1), scores_now)
            for rows_by_head, lead in ((q_rows, Q_TRANSPOSE_LEAD), (k_rows, K_TRANSPOSE_LEAD)):
                head = head_starting(step + lead) if step > 0 else head_starting(step + lead - 1)
                if head is not None:
                    for j in range(TILES):
                        transpose_words(rows_by_head, head, j)
            if scores_next is not None and scores_next >= BIAS_FIRST_FROM:
                for t in range(TILES):
                    bias_transpose(scores_next, t)
            if prob_now is not None:
                for u in range(2):
                    transpose_prob(prob_now, u)
            if step == 0:
                transpose_bias(2)
                for t in range(TILES):
                    bias_transpose(scores_now, t)
                transpose_bias(3)

            run(exponential, tile_behind(step, EXP_LAG))
            if step == 0:
                copy_bias(2)
            run(copy_prob, pair_behind(step, PROB_COPY_LAG))
            run(copy_q, head_starting(step + Q_COPY_LEAD))

            run(normalise, pair_behind(step, NORM_LAG))
            run(row_max, tile_behind(step, MAX_LAG))
            if step == 1:
                copy_bias(3)
            run(copy_k, head_starting(step + K_COPY_LEAD))
            run(store, pair_behind(step, OUT_LAG))
            run(quantise_prob, pair_behind(step, PROB_QUANT_LAG))
            run(quantise_v, head_for_v(step, V_QUANT_LAG))
            run(regroup_v, head_for_v(step, V_REGROUP_LAG))
